import numpy as np
import ml_dtypes


def mxq(x, axis, fmt="e4m3"):
    dtype, down = {"e4m3": (ml_dtypes.float8_e4m3fn, 7), "e5m2": (ml_dtypes.float8_e5m2, 14)}[fmt]
    v = np.moveaxis(np.asarray(x, np.float32).astype(ml_dtypes.bfloat16).astype(np.float64), axis, -1)
    blocks = v.reshape(v.shape[:-1] + (-1, 32))
    amax = np.abs(blocks).max(-1, keepdims=True)
    byte = np.maximum(np.where(amax > 0, np.frexp(amax)[1] - 1 + 127, 0) - down, 1)
    scale = np.exp2(byte - 127.0)
    codes = (blocks / scale).astype(np.float32).astype(dtype).astype(np.float64)
    return np.moveaxis((codes * scale).reshape(v.shape), -1, axis)


WIDE = False


def mx_kscale(k):
    if not WIDE:
        return np.ones(k)
    levels = np.array([10, -10, 5, -5, 0])
    a = np.random.permutation(np.resize(levels, k // 512 * 4)).reshape(k // 512, 4)
    idx = np.arange(k)
    return np.exp2(a[idx // 512, idx % 128 // 32])


BF16 = ml_dtypes.bfloat16


def bf(x):
    return np.asarray(x, np.float32).astype(BF16)


def f64(x):
    return np.asarray(x).astype(np.float64)


B, N, D, DO, H, HID = 48, 128, 512, 512, 8, 256
EPS = 1e-5


def gelu_tanh(v):
    return 0.5 * v * (1.0 + np.tanh(np.sqrt(2.0 / np.pi) * (v + 0.044715 * v**3)))


def layer_norm(v, g, b):
    m = v.mean(-1, keepdims=True)
    var = v.var(-1, keepdims=True)
    return (v - m) * (1.0 / np.sqrt(var + EPS)) * g + b


def setup_inputs():
    t = mx_kscale(D)
    return {
        "x": bf(np.random.standard_normal((B, N, D))),
        "h2": bf(np.random.standard_normal((B, N, D)) * 0.7),
        "xfeat_w": bf(np.random.standard_normal((D, D)) / np.sqrt(D)),
        "xfeat_b": bf(np.random.standard_normal(D) * 0.1),
        "pos_mix": bf(np.random.standard_normal((N, N)) * 0.5 / np.sqrt(N)),
        "ln2_g": bf((1.0 + 0.1 * np.random.standard_normal(D)) * t),
        "ln2_b": bf(0.1 * np.random.standard_normal(D) * t),
        "mlp_w1": bf(np.random.standard_normal((D, HID)) / np.sqrt(D) / t[:, None]),
        "mlp_b1": bf(0.1 * np.random.standard_normal(HID)),
    }


def reference(x, h2, xfeat_w, xfeat_b, pos_mix, ln2_g, ln2_b, mlp_w1, mlp_b1):
    xf = (mxq(f64(h2), 2, "e4m3") @ mxq(f64(xfeat_w), 0, "e4m3")) + f64(xfeat_b) + f64(pos_mix) @ f64(h2)
    x1 = f64(x) + xf
    h = layer_norm(x1, f64(ln2_g), f64(ln2_b))
    return gelu_tanh((mxq(h, 2, "e4m3") @ mxq(f64(mlp_w1), 0, "e4m3")) + f64(mlp_b1))

@@ -1,0 +1,251 @@
+from contextlib import ExitStack
+
+import concourse.mybir as mybir
+from concourse.masks import make_identity
+
+F32 = mybir.dt.float32
+BF16 = mybir.dt.bfloat16
+U32 = mybir.dt.uint32
+U8 = mybir.dt.uint8
+FP8X4 = mybir.dt.float8_e4m3fn_x4
+ALU = mybir.AluOpType
+ACT = mybir.ActivationFunctionType
+
+B, N, D, HID = 48, 128, 512, 256
+P = 128
+QUAD = 4
+NQ = B // QUAD
+EPS = 1e-5
+FLOPS = 2 * B * N * (D * D + N * D + D * HID)
+LOAD_AHEAD = 5
+
+
+def tile_gatblock_pb_t_kernel(
+    tc, x, h2, xfeat_w, xfeat_b, pos_mix, ln2_g, ln2_b, mlp_w1, mlp_b1, out
+):
+    nc = tc.nc
+    x_v = x.rearrange("b n f -> n b f")
+    h2_v = h2.rearrange("b n f -> n b f")
+    out_v = out.rearrange("b n j -> n b j")
+
+    with ExitStack() as ctx:
+        const = ctx.enter_context(tc.tile_pool(name="const", bufs=1))
+        xin = ctx.enter_context(tc.tile_pool(name="xin", bufs=LOAD_AHEAD + 1))
+        hin = ctx.enter_context(tc.tile_pool(name="hin", bufs=LOAD_AHEAD + 1))
+        xbp = ctx.enter_context(tc.tile_pool(name="xbp", bufs=4))
+        zp = ctx.enter_context(tc.tile_pool(name="zp", bufs=2))
+        work = ctx.enter_context(tc.tile_pool(name="work", bufs=2))
+        stat = ctx.enter_context(tc.tile_pool(name="stat", bufs=4))
+        ps_t1 = ctx.enter_context(tc.psum_pool(name="ps_t1", bufs=1))
+        ps_mx = ctx.enter_context(tc.psum_pool(name="ps_mx", bufs=2))
+        ps_pos = ctx.enter_context(tc.psum_pool(name="ps_pos", bufs=2))
+        ps_zt = ctx.enter_context(tc.psum_pool(name="ps_zt", bufs=2))
+        ps_m2 = ctx.enter_context(tc.psum_pool(name="ps_m2", bufs=1))
+
+        xq = {}
+        hq = {}
+
+        def load(q):
+            hq[q] = hin.tile([P, QUAD * D], BF16, name="hq", tag="hq")
+            nc.sync.dma_start(
+                out=hq[q][:].rearrange("p (s f) -> p s f", s=QUAD),
+                in_=h2_v[:, q * QUAD : (q + 1) * QUAD, :],
+            )
+            xq[q] = xin.tile([P, QUAD * D], BF16, name="xq", tag="xq")
+            nc.sync.dma_start(
+                out=xq[q][:].rearrange("p (s f) -> p s f", s=QUAD),
+                in_=x_v[:, q * QUAD : (q + 1) * QUAD, :],
+            )
+
+        warm = const.tile([P, 1], F32, name="warm")
+        nc.vector.memset(warm[:], 0.0)
+        nc.scalar.activation(out=warm[:], in_=warm[:], func=ACT.Gelu_apprx_tanh)
+
+        wraw = const.tile([P, 4, D], BF16, name="wraw")
+        nc.sync.dma_start(
+            out=wraw[:].rearrange("p (u e) c -> p u (e c)", u=2),
+            in_=xfeat_w.rearrange("(u p e) c -> p u (e c)", u=2, e=2),
+        )
+        pm = const.tile([P, P], BF16, name="pm")
+        nc.sync.dma_start(out=pm[:], in_=pos_mix)
+        load(0)
+        w1raw = const.tile([P, 4, HID], BF16, name="w1raw")
+        nc.sync.dma_start(out=w1raw[:], in_=mlp_w1.rearrange("(t p) c -> p t c", p=P))
+
+        beta = const.tile([P, D], BF16, name="beta")
+        nc.scalar.dma_start(out=beta[:], in_=xfeat_b.partition_broadcast(P))
+        gbrow = const.tile([P, P], BF16, name="gbrow")
+        nc.vector.memset(gbrow[:], 0.0)
+        nc.scalar.dma_start(out=gbrow[0:4, :], in_=ln2_g.rearrange("(t p) -> t p", p=P))
+        nc.scalar.dma_start(out=gbrow[4:8, :], in_=ln2_b.rearrange("(t p) -> t p", p=P))
+        b1bc = const.tile([P, HID], BF16, name="b1bc")
+        nc.scalar.dma_start(out=b1bc[:], in_=mlp_b1.partition_broadcast(P))
+
+        for q in range(1, LOAD_AHEAD):
+            load(q)
+
+        ident_f = const.tile([P, P], F32, name="ident_f")
+        make_identity(nc, ident_f[:])
+        ident_b = const.tile([P, P], BF16, name="ident_b")
+        make_identity(nc, ident_b[:])
+        mhalf = const.tile([P, QUAD], F32, name="mhalf")
+        nc.vector.memset(mhalf[:], -0.5)
+
+        wgrp = const.tile([P, D, 4], BF16, name="wgrp", align_bytes=64)
+        nc.vector.tensor_copy(out=wgrp[:], in_=wraw[:].rearrange("p t c -> p c t"))
+        wcod = const.tile([P, D], U32, name="wcod", align_bytes=64)
+        wsc = const.tile([P, D], U8, name="wsc", align_bytes=64)
+        nc.vector.quantize_mx(
+            out=wcod[:].bitcast(FP8X4), scales=wsc[:], in_=wgrp[:].rearrange("p c t -> p (c t)")
+        )
+        w1grp = const.tile([P, HID, 4], BF16, name="w1grp", align_bytes=64)
+        nc.vector.tensor_copy(out=w1grp[:], in_=w1raw[:].rearrange("p t c -> p c t"))
+        w1cod = const.tile([P, HID], U32, name="w1cod", align_bytes=64)
+        w1sc = const.tile([P, HID], U8, name="w1sc", align_bytes=64)
+        nc.vector.quantize_mx(
+            out=w1cod[:].bitcast(FP8X4), scales=w1sc[:], in_=w1grp[:].rearrange("p c t -> p (c t)")
+        )
+
+        pmT_ps = ps_t1.tile([P, P], BF16, name="pmT_ps", tag="t1")
+        nc.tensor.transpose(pmT_ps[:], pm[:], ident_b[:])
+        pmT = const.tile([P, P], BF16, name="pmT")
+        nc.vector.tensor_copy(out=pmT[:], in_=pmT_ps[:])
+        gb_ps = ps_t1.tile([P, P], BF16, name="gb_ps", tag="t1")
+        nc.tensor.transpose(gb_ps[:], gbrow[:], ident_b[:])
+        gT = const.tile([P, 4], F32, name="gT")
+        nc.vector.tensor_copy(out=gT[:], in_=gb_ps[:, 0:4])
+        bT = const.tile([P, 4], F32, name="bT")
+        nc.vector.tensor_copy(out=bT[:], in_=gb_ps[:, 4:8])
+
+        for q in range(NQ):
+            if q + LOAD_AHEAD < NQ:
+                load(q + LOAD_AHEAD)
+            h_t = hq[q]
+            x_t = xq[q]
+
+            xb = xbp.tile([P, QUAD, D], F32, name="xb", tag="xb")
+            nc.gpsimd.tensor_tensor(
+                out=xb[:],
+                in0=x_t[:].rearrange("p (s f) -> p s f", s=QUAD),
+                in1=beta[:].unsqueeze(1).to_broadcast([P, QUAD, D]),
+                op=ALU.add,
+            )
+
+            g1 = work.tile([P, QUAD * D], BF16, name="g1", tag="g1", align_bytes=64)
+            h_w = h_t[:].bitcast(F32)
+            g1_w = g1[:].bitcast(F32)
+            for pr in range(2):
+                t1 = ps_t1.tile([P, 2, 2, P], F32, name="t1", tag="t1")
+                for s in range(2):
+                    for u in range(2):
+                        c0 = (2 * pr + s) * (D // 2) + u * P
+                        nc.tensor.transpose(t1[:, s, u, :], h_w[:, c0 : c0 + P], ident_f[:])
+                nc.scalar.copy(
+                    out=g1_w[:, pr * D : (pr + 1) * D].rearrange("p (s n u) -> p s n u", s=2, u=2),
+                    in_=t1[:].rearrange("p s u n -> p s n u"),
+                )
+            c1 = work.tile([P, QUAD * P], U32, name="c1", tag="c1", align_bytes=64)
+            s1 = work.tile([P, QUAD * P], U8, name="s1", tag="s1", align_bytes=64)
+            nc.vector.quantize_mx(out=c1[:].bitcast(FP8X4), scales=s1[:], in_=g1[:])
+
+            sums = stat.tile([P, QUAD], F32, name="sums", tag="sums")
+            for s in range(QUAD):
+                mx = ps_mx.tile([P, D], F32, name="mx", tag="mx")
+                nc.tensor.matmul_mx(
+                    out=mx[:],
+                    lhsT=c1[:, s * P : (s + 1) * P].bitcast(FP8X4),
+                    lhsT_scale=s1[:, s * P : (s + 1) * P],
+                    rhs=wcod[:].bitcast(FP8X4),
+                    rhs_scale=wsc[:],
+                    start=True,
+                    stop=True,
+                )
+                pos = ps_pos.tile([P, D], F32, name="pos", tag="pos")
+                nc.tensor.matmul(
+                    out=pos[:], lhsT=pmT[:], rhs=h_t[:, s * D : (s + 1) * D], start=True, stop=True
+                )
+                nc.vector.tensor_tensor(out=xb[:, s, :], in0=mx[:], in1=xb[:, s, :], op=ALU.add)
+                nc.vector.scalar_tensor_tensor(
+                    out=xb[:, s, :],
+                    in0=pos[:],
+                    scalar=1.0,
+                    in1=xb[:, s, :],
+                    op0=ALU.mult,
+                    op1=ALU.add,
+                    accum_out=sums[:, s : s + 1],
+                )
+            nm = stat.tile([P, QUAD], F32, name="nm", tag="nm")
+            nc.vector.tensor_scalar(
+                out=nm[:], in0=sums[:], scalar1=-1.0 / D, scalar2=None, op0=ALU.mult
+            )
+            ssq = stat.tile([P, QUAD], F32, name="ssq", tag="ssq")
+            for s in range(QUAD):
+                junk = work.tile([P, D], BF16, name="junk", tag="junk")
+                nc.scalar.activation(
+                    out=junk[:],
+                    in_=xb[:, s, :],
+                    func=ACT.Square,
+                    bias=nm[:, s : s + 1],
+                    scale=1.0,
+                    accum_out=ssq[:, s : s + 1],
+                )
+            var = stat.tile([P, QUAD], F32, name="var", tag="var")
+            nc.gpsimd.tensor_scalar(
+                out=var[:], in0=ssq[:], scalar1=1.0 / D, scalar2=EPS, op0=ALU.mult, op1=ALU.add
+            )
+            rstd = stat.tile([P, QUAD], F32, name="rstd", tag="rstd")
+            nc.gpsimd.tensor_tensor(out=rstd[:], in0=var[:], in1=mhalf[:], op=ALU.pow)
+            z = zp.tile([P, QUAD, D], F32, name="z", tag="z")
+            for s in range(QUAD):
+                nc.gpsimd.tensor_scalar(
+                    out=z[:, s, :],
+                    in0=xb[:, s, :],
+                    scalar1=nm[:, s : s + 1],
+                    scalar2=rstd[:, s : s + 1],
+                    op0=ALU.add,
+                    op1=ALU.mult,
+                )
+
+            planes = work.tile([P, 4, QUAD * P], BF16, name="planes", tag="planes")
+            for t in range(4):
+                zt = ps_zt.tile([P, QUAD, P], F32, name="zt", tag="zt")
+                for s in range(QUAD):
+                    nc.tensor.transpose(zt[:, s, :], z[:, s, t * P : (t + 1) * P], ident_f[:])
+                nc.scalar.activation(
+                    out=planes[:, t, :],
+                    in_=zt[:].rearrange("p s n -> p (s n)"),
+                    func=ACT.Identity,
+                    bias=bT[:, t : t + 1],
+                    scale=gT[:, t : t + 1],
+                )
+            g2 = work.tile([P, QUAD * P, 4], BF16, name="g2", tag="g2", align_bytes=64)
+            nc.vector.tensor_copy(out=g2[:], in_=planes[:].rearrange("p t w -> p w t"))
+            c2 = work.tile([P, QUAD * P], U32, name="c2", tag="c2", align_bytes=64)
+            s2 = work.tile([P, QUAD * P], U8, name="s2", tag="s2", align_bytes=64)
+            nc.vector.quantize_mx(
+                out=c2[:].bitcast(FP8X4), scales=s2[:], in_=g2[:].rearrange("p w t -> p (w t)")
+            )
+
+            o = work.tile([P, QUAD, HID], F32, name="o", tag="o")
+            for pr in range(2):
+                m2 = ps_m2.tile([P, 2, HID], F32, name="m2", tag="m2")
+                for s in range(2):
+                    w0 = (2 * pr + s) * P
+                    nc.tensor.matmul_mx(
+                        out=m2[:, s, :],
+                        lhsT=c2[:, w0 : w0 + P].bitcast(FP8X4),
+                        lhsT_scale=s2[:, w0 : w0 + P],
+                        rhs=w1cod[:].bitcast(FP8X4),
+                        rhs_scale=w1sc[:],
+                        start=True,
+                        stop=True,
+                    )
+                nc.vector.tensor_tensor(
+                    out=o[:, 2 * pr : 2 * pr + 2, :],
+                    in0=m2[:],
+                    in1=b1bc[:].unsqueeze(1).to_broadcast([P, 2, HID]),
+                    op=ALU.add,
+                )
+            res = work.tile([P, QUAD, HID], F32, name="res", tag="res")
+            nc.scalar.activation(out=res[:], in_=o[:], func=ACT.Gelu_apprx_tanh)
+            nc.sync.dma_start(out=out_v[:, q * QUAD : (q + 1) * QUAD, :], in_=res[:])

@@ -15,9 +15,11 @@ B, N, D, HID = 48, 128, 512, 256
 P = 128
 QUAD = 4
 NQ = B // QUAD
+NPAIR = B // 2
 EPS = 1e-5
 FLOPS = 2 * B * N * (D * D + N * D + D * HID)
 LOAD_AHEAD = 5
+RG_V = 384
 
 
 def tile_gatblock_pb_t_kernel(
@@ -32,20 +34,24 @@ def tile_gatblock_pb_t_kernel(
         const = ctx.enter_context(tc.tile_pool(name="const", bufs=1))
         xin = ctx.enter_context(tc.tile_pool(name="xin", bufs=LOAD_AHEAD + 1))
         hin = ctx.enter_context(tc.tile_pool(name="hin", bufs=LOAD_AHEAD + 1))
-        xbp = ctx.enter_context(tc.tile_pool(name="xbp", bufs=4))
+        xbp = ctx.enter_context(tc.tile_pool(name="xbp", bufs=3))
         zp = ctx.enter_context(tc.tile_pool(name="zp", bufs=2))
-        work = ctx.enter_context(tc.tile_pool(name="work", bufs=2))
+        w3 = ctx.enter_context(tc.tile_pool(name="w3", bufs=3))
+        w2 = ctx.enter_context(tc.tile_pool(name="w2", bufs=2))
         stat = ctx.enter_context(tc.tile_pool(name="stat", bufs=4))
-        ps_t1 = ctx.enter_context(tc.psum_pool(name="ps_t1", bufs=1))
+        ps_tr = ctx.enter_context(tc.psum_pool(name="ps_tr", bufs=3))
         ps_mx = ctx.enter_context(tc.psum_pool(name="ps_mx", bufs=2))
         ps_pos = ctx.enter_context(tc.psum_pool(name="ps_pos", bufs=2))
-        ps_zt = ctx.enter_context(tc.psum_pool(name="ps_zt", bufs=2))
         ps_m2 = ctx.enter_context(tc.psum_pool(name="ps_m2", bufs=1))
+        ctx.enter_context(tc.manual_schedule())
 
-        xq = {}
-        hq = {}
+        xq, hq, t1, g1, c1, s1 = {}, {}, {}, {}, {}, {}
+        mx, pos, xb, sums, nm, ssq, rstd = {}, {}, {}, {}, {}, {}, {}
+        z, zt, planes, g2, c2, s2, m2, o = {}, {}, {}, {}, {}, {}, {}, {}
 
         def load(q):
+            if not 0 <= q < NQ:
+                return
             hq[q] = hin.tile([P, QUAD * D], BF16, name="hq", tag="hq")
             nc.sync.dma_start(
                 out=hq[q][:].rearrange("p (s f) -> p s f", s=QUAD),
@@ -57,195 +63,317 @@ def tile_gatblock_pb_t_kernel(
                 in_=x_v[:, q * QUAD : (q + 1) * QUAD, :],
             )
 
-        warm = const.tile([P, 1], F32, name="warm")
-        nc.vector.memset(warm[:], 0.0)
-        nc.scalar.activation(out=warm[:], in_=warm[:], func=ACT.Gelu_apprx_tanh)
-
         wraw = const.tile([P, 4, D], BF16, name="wraw")
         nc.sync.dma_start(
             out=wraw[:].rearrange("p (u e) c -> p u (e c)", u=2),
             in_=xfeat_w.rearrange("(u p e) c -> p u (e c)", u=2, e=2),
         )
         pm = const.tile([P, P], BF16, name="pm")
-        nc.sync.dma_start(out=pm[:], in_=pos_mix)
-        load(0)
-        w1raw = const.tile([P, 4, HID], BF16, name="w1raw")
-        nc.sync.dma_start(out=w1raw[:], in_=mlp_w1.rearrange("(t p) c -> p t c", p=P))
-
-        beta = const.tile([P, D], BF16, name="beta")
-        nc.scalar.dma_start(out=beta[:], in_=xfeat_b.partition_broadcast(P))
+        nc.scalar.dma_start(out=pm[:], in_=pos_mix)
         gbrow = const.tile([P, P], BF16, name="gbrow")
         nc.vector.memset(gbrow[:], 0.0)
         nc.scalar.dma_start(out=gbrow[0:4, :], in_=ln2_g.rearrange("(t p) -> t p", p=P))
         nc.scalar.dma_start(out=gbrow[4:8, :], in_=ln2_b.rearrange("(t p) -> t p", p=P))
+        nc.scalar.dma_start(out=gbrow[8:12, :], in_=xfeat_b.rearrange("(t p) -> t p", p=P))
         b1bc = const.tile([P, HID], BF16, name="b1bc")
         nc.scalar.dma_start(out=b1bc[:], in_=mlp_b1.partition_broadcast(P))
+        warm = const.tile([P, 1], F32, name="warm")
+        nc.vector.memset(warm[:], 0.0)
+        nc.scalar.activation(out=warm[:], in_=warm[:], func=ACT.Gelu_apprx_tanh)
 
-        for q in range(1, LOAD_AHEAD):
+        load(0)
+        load(1)
+        w1raw = const.tile([P, 4, HID], BF16, name="w1raw")
+        nc.sync.dma_start(out=w1raw[:], in_=mlp_w1.rearrange("(t p) c -> p t c", p=P))
+        for q in range(2, LOAD_AHEAD):
             load(q)
 
         ident_f = const.tile([P, P], F32, name="ident_f")
         make_identity(nc, ident_f[:])
         ident_b = const.tile([P, P], BF16, name="ident_b")
         make_identity(nc, ident_b[:])
-        mhalf = const.tile([P, QUAD], F32, name="mhalf")
+        mhalf = const.tile([P, 2], F32, name="mhalf")
         nc.vector.memset(mhalf[:], -0.5)
 
+        def regroup(eng_copy, dst, src):
+            eng_copy(
+                out=dst.rearrange("p (c i) t -> p c t i", i=4),
+                in_=src.rearrange("p t (c i) -> p c t i", i=4),
+            )
+
         wgrp = const.tile([P, D, 4], BF16, name="wgrp", align_bytes=64)
-        nc.vector.tensor_copy(out=wgrp[:], in_=wraw[:].rearrange("p t c -> p c t"))
+        regroup(nc.vector.tensor_copy, wgrp[:], wraw[:])
         wcod = const.tile([P, D], U32, name="wcod", align_bytes=64)
         wsc = const.tile([P, D], U8, name="wsc", align_bytes=64)
         nc.vector.quantize_mx(
             out=wcod[:].bitcast(FP8X4), scales=wsc[:], in_=wgrp[:].rearrange("p c t -> p (c t)")
         )
-        w1grp = const.tile([P, HID, 4], BF16, name="w1grp", align_bytes=64)
-        nc.vector.tensor_copy(out=w1grp[:], in_=w1raw[:].rearrange("p t c -> p c t"))
-        w1cod = const.tile([P, HID], U32, name="w1cod", align_bytes=64)
-        w1sc = const.tile([P, HID], U8, name="w1sc", align_bytes=64)
-        nc.vector.quantize_mx(
-            out=w1cod[:].bitcast(FP8X4), scales=w1sc[:], in_=w1grp[:].rearrange("p c t -> p (c t)")
-        )
 
-        pmT_ps = ps_t1.tile([P, P], BF16, name="pmT_ps", tag="t1")
+        pmT_ps = ps_tr.tile([P, P], BF16, name="pmT_ps", tag="tr")
         nc.tensor.transpose(pmT_ps[:], pm[:], ident_b[:])
         pmT = const.tile([P, P], BF16, name="pmT")
         nc.vector.tensor_copy(out=pmT[:], in_=pmT_ps[:])
-        gb_ps = ps_t1.tile([P, P], BF16, name="gb_ps", tag="t1")
+        gb_ps = ps_tr.tile([P, P], BF16, name="gb_ps", tag="tr")
         nc.tensor.transpose(gb_ps[:], gbrow[:], ident_b[:])
         gT = const.tile([P, 4], F32, name="gT")
         nc.vector.tensor_copy(out=gT[:], in_=gb_ps[:, 0:4])
         bT = const.tile([P, 4], F32, name="bT")
         nc.vector.tensor_copy(out=bT[:], in_=gb_ps[:, 4:8])
+        betacol = const.tile([P, 4, P], F32, name="betacol")
+        nc.vector.tensor_copy(
+            out=betacol[:], in_=gb_ps[:, 8:12].unsqueeze(2).to_broadcast([P, 4, P])
+        )
 
-        for q in range(NQ):
-            if q + LOAD_AHEAD < NQ:
-                load(q + LOAD_AHEAD)
-            h_t = hq[q]
-            x_t = xq[q]
+        w1cod = const.tile([P, HID], U32, name="w1cod", align_bytes=64)
+        w1sc = const.tile([P, HID], U8, name="w1sc", align_bytes=64)
 
-            xb = xbp.tile([P, QUAD, D], F32, name="xb", tag="xb")
-            nc.gpsimd.tensor_tensor(
-                out=xb[:],
-                in0=x_t[:].rearrange("p (s f) -> p s f", s=QUAD),
-                in1=beta[:].unsqueeze(1).to_broadcast([P, QUAD, D]),
-                op=ALU.add,
+        def quantise_w1():
+            w1grp = const.tile([P, HID, 4], BF16, name="w1grp", align_bytes=64)
+            regroup(nc.vector.tensor_copy, w1grp[:], w1raw[:])
+            nc.vector.quantize_mx(
+                out=w1cod[:].bitcast(FP8X4),
+                scales=w1sc[:],
+                in_=w1grp[:].rearrange("p c t -> p (c t)"),
             )
 
-            g1 = work.tile([P, QUAD * D], BF16, name="g1", tag="g1", align_bytes=64)
-            h_w = h_t[:].bitcast(F32)
-            g1_w = g1[:].bitcast(F32)
-            for pr in range(2):
-                t1 = ps_t1.tile([P, 2, 2, P], F32, name="t1", tag="t1")
-                for s in range(2):
-                    for u in range(2):
-                        c0 = (2 * pr + s) * (D // 2) + u * P
-                        nc.tensor.transpose(t1[:, s, u, :], h_w[:, c0 : c0 + P], ident_f[:])
-                nc.scalar.copy(
-                    out=g1_w[:, pr * D : (pr + 1) * D].rearrange("p (s n u) -> p s n u", s=2, u=2),
-                    in_=t1[:].rearrange("p s u n -> p s n u"),
-                )
-            c1 = work.tile([P, QUAD * P], U32, name="c1", tag="c1", align_bytes=64)
-            s1 = work.tile([P, QUAD * P], U8, name="s1", tag="s1", align_bytes=64)
-            nc.vector.quantize_mx(out=c1[:].bitcast(FP8X4), scales=s1[:], in_=g1[:])
+        def h2_transposes(j):
+            if not 0 <= j < NPAIR:
+                return
+            h_w = hq[j // 2][:].bitcast(F32)
+            t1[j] = ps_tr.tile([P, 2, 2, P], F32, name="t1", tag="tr")
+            for s in range(2):
+                for u in range(2):
+                    c0 = (2 * (j % 2) + s) * (D // 2) + u * P
+                    nc.tensor.transpose(t1[j][:, s, u, :], h_w[:, c0 : c0 + P], ident_f[:])
 
-            sums = stat.tile([P, QUAD], F32, name="sums", tag="sums")
-            for s in range(QUAD):
-                mx = ps_mx.tile([P, D], F32, name="mx", tag="mx")
-                nc.tensor.matmul_mx(
-                    out=mx[:],
-                    lhsT=c1[:, s * P : (s + 1) * P].bitcast(FP8X4),
-                    lhsT_scale=s1[:, s * P : (s + 1) * P],
-                    rhs=wcod[:].bitcast(FP8X4),
-                    rhs_scale=wsc[:],
+        def h2_copy(j):
+            if not 0 <= j < NPAIR:
+                return
+            q = j // 2
+            if j % 2 == 0:
+                g1[q] = w3.tile([P, QUAD * D], BF16, name="g1", tag="g1", align_bytes=64)
+            g1_w = g1[q][:].bitcast(F32)
+            nc.scalar.copy(
+                out=g1_w[:, (j % 2) * D : (j % 2 + 1) * D].rearrange(
+                    "p (s n u) -> p s n u", s=2, u=2
+                ),
+                in_=t1[j][:].rearrange("p s u n -> p s n u"),
+            )
+
+        def h2_quantise(q):
+            if not 0 <= q < NQ:
+                return
+            c1[q] = w3.tile([P, QUAD * P], U32, name="c1", tag="c1", align_bytes=64)
+            s1[q] = w3.tile([P, QUAD * P], U8, name="s1", tag="s1", align_bytes=64)
+            nc.vector.quantize_mx(out=c1[q][:].bitcast(FP8X4), scales=s1[q][:], in_=g1[q][:])
+
+        def feat_matmul(s):
+            if not 0 <= s < B:
+                return
+            q, i = s // QUAD, s % QUAD
+            mx[s] = ps_mx.tile([P, D], F32, name="mx", tag="mx")
+            nc.tensor.matmul_mx(
+                out=mx[s][:],
+                lhsT=c1[q][:, i * P : (i + 1) * P].bitcast(FP8X4),
+                lhsT_scale=s1[q][:, i * P : (i + 1) * P],
+                rhs=wcod[:].bitcast(FP8X4),
+                rhs_scale=wsc[:],
+                start=True,
+                stop=True,
+            )
+
+        def pos_matmul(s):
+            if not 0 <= s < B:
+                return
+            q, i = s // QUAD, s % QUAD
+            pos[s] = ps_pos.tile([P, D], F32, name="pos", tag="pos")
+            for c in range(4):
+                nc.tensor.matmul(
+                    out=pos[s][:, c * P : (c + 1) * P],
+                    lhsT=pmT[:],
+                    rhs=hq[q][:, i * D + c * P : i * D + (c + 1) * P],
                     start=True,
+                    stop=False,
+                )
+                nc.tensor.matmul(
+                    out=pos[s][:, c * P : (c + 1) * P],
+                    lhsT=betacol[:, c, :],
+                    rhs=ident_f[:],
+                    is_transpose=True,
+                    start=False,
                     stop=True,
                 )
-                pos = ps_pos.tile([P, D], F32, name="pos", tag="pos")
-                nc.tensor.matmul(
-                    out=pos[:], lhsT=pmT[:], rhs=h_t[:, s * D : (s + 1) * D], start=True, stop=True
-                )
-                nc.vector.tensor_tensor(out=xb[:, s, :], in0=mx[:], in1=xb[:, s, :], op=ALU.add)
-                nc.vector.scalar_tensor_tensor(
-                    out=xb[:, s, :],
-                    in0=pos[:],
-                    scalar=1.0,
-                    in1=xb[:, s, :],
-                    op0=ALU.mult,
-                    op1=ALU.add,
-                    accum_out=sums[:, s : s + 1],
-                )
-            nm = stat.tile([P, QUAD], F32, name="nm", tag="nm")
-            nc.vector.tensor_scalar(
-                out=nm[:], in0=sums[:], scalar1=-1.0 / D, scalar2=None, op0=ALU.mult
+
+        def residual(s):
+            if not 0 <= s < B:
+                return
+            q, i, j = s // QUAD, s % QUAD, s // 2
+            if i == 0:
+                xb[q] = xbp.tile([P, QUAD, D], F32, name="xb", tag="xb")
+            if s % 2 == 0:
+                sums[j] = stat.tile([P, 2], F32, name="sums", tag="sums")
+            nc.vector.tensor_tensor(
+                out=xb[q][:, i, :], in0=mx[s][:], in1=xq[q][:, i * D : (i + 1) * D], op=ALU.add
             )
-            ssq = stat.tile([P, QUAD], F32, name="ssq", tag="ssq")
-            for s in range(QUAD):
-                junk = work.tile([P, D], BF16, name="junk", tag="junk")
+            nc.vector.scalar_tensor_tensor(
+                out=xb[q][:, i, :],
+                in0=pos[s][:],
+                scalar=1.0,
+                in1=xb[q][:, i, :],
+                op0=ALU.mult,
+                op1=ALU.add,
+                accum_out=sums[j][:, s % 2 : s % 2 + 1],
+            )
+
+        def squares(j):
+            if not 0 <= j < NPAIR:
+                return
+            nm[j] = stat.tile([P, 2], F32, name="nm", tag="nm")
+            nc.scalar.activation(out=nm[j][:], in_=sums[j][:], func=ACT.Copy, scale=-1.0 / D)
+            ssq[j] = stat.tile([P, 2], F32, name="ssq", tag="ssq")
+            for e in range(2):
+                s = 2 * j + e
+                junk = w2.tile([P, D], BF16, name="junk", tag="junk")
                 nc.scalar.activation(
                     out=junk[:],
-                    in_=xb[:, s, :],
+                    in_=xb[s // QUAD][:, s % QUAD, :],
                     func=ACT.Square,
-                    bias=nm[:, s : s + 1],
+                    bias=nm[j][:, e : e + 1],
                     scale=1.0,
-                    accum_out=ssq[:, s : s + 1],
+                    accum_out=ssq[j][:, e : e + 1],
                 )
-            var = stat.tile([P, QUAD], F32, name="var", tag="var")
+
+        def normalise(j):
+            if not 0 <= j < NPAIR:
+                return
+            q = j // 2
+            var = stat.tile([P, 2], F32, name="var", tag="var")
             nc.gpsimd.tensor_scalar(
-                out=var[:], in0=ssq[:], scalar1=1.0 / D, scalar2=EPS, op0=ALU.mult, op1=ALU.add
+                out=var[:], in0=ssq[j][:], scalar1=1.0 / D, scalar2=EPS, op0=ALU.mult, op1=ALU.add
             )
-            rstd = stat.tile([P, QUAD], F32, name="rstd", tag="rstd")
-            nc.gpsimd.tensor_tensor(out=rstd[:], in0=var[:], in1=mhalf[:], op=ALU.pow)
-            z = zp.tile([P, QUAD, D], F32, name="z", tag="z")
-            for s in range(QUAD):
+            rstd[j] = stat.tile([P, 2], F32, name="rstd", tag="rstd")
+            nc.gpsimd.tensor_tensor(out=rstd[j][:], in0=var[:], in1=mhalf[:], op=ALU.pow)
+            if j % 2 == 0:
+                z[q] = zp.tile([P, QUAD, D], F32, name="z", tag="z")
+            for e in range(2):
+                i = 2 * (j % 2) + e
                 nc.gpsimd.tensor_scalar(
-                    out=z[:, s, :],
-                    in0=xb[:, s, :],
-                    scalar1=nm[:, s : s + 1],
-                    scalar2=rstd[:, s : s + 1],
+                    out=z[q][:, i, :],
+                    in0=xb[q][:, i, :],
+                    scalar1=nm[j][:, e : e + 1],
+                    scalar2=rstd[j][:, e : e + 1],
                     op0=ALU.add,
                     op1=ALU.mult,
                 )
 
-            planes = work.tile([P, 4, QUAD * P], BF16, name="planes", tag="planes")
-            for t in range(4):
-                zt = ps_zt.tile([P, QUAD, P], F32, name="zt", tag="zt")
-                for s in range(QUAD):
-                    nc.tensor.transpose(zt[:, s, :], z[:, s, t * P : (t + 1) * P], ident_f[:])
-                nc.scalar.activation(
-                    out=planes[:, t, :],
-                    in_=zt[:].rearrange("p s n -> p (s n)"),
-                    func=ACT.Identity,
-                    bias=bT[:, t : t + 1],
-                    scale=gT[:, t : t + 1],
-                )
-            g2 = work.tile([P, QUAD * P, 4], BF16, name="g2", tag="g2", align_bytes=64)
-            nc.vector.tensor_copy(out=g2[:], in_=planes[:].rearrange("p t w -> p w t"))
-            c2 = work.tile([P, QUAD * P], U32, name="c2", tag="c2", align_bytes=64)
-            s2 = work.tile([P, QUAD * P], U8, name="s2", tag="s2", align_bytes=64)
-            nc.vector.quantize_mx(
-                out=c2[:].bitcast(FP8X4), scales=s2[:], in_=g2[:].rearrange("p w t -> p (w t)")
+        def z_transposes(q, t):
+            if not 0 <= q < NQ:
+                return
+            zt[q, t] = ps_tr.tile([P, QUAD, P], F32, name="zt", tag="tr")
+            for i in range(QUAD):
+                nc.tensor.transpose(zt[q, t][:, i, :], z[q][:, i, t * P : (t + 1) * P], ident_f[:])
+
+        def gain_bias(q, t):
+            if not 0 <= q < NQ:
+                return
+            if t == 0:
+                planes[q] = w2.tile([P, 4, QUAD * P], BF16, name="planes", tag="planes")
+            nc.scalar.activation(
+                out=planes[q][:, t, :],
+                in_=zt[q, t][:].rearrange("p s n -> p (s n)"),
+                func=ACT.Identity,
+                bias=bT[:, t : t + 1],
+                scale=gT[:, t : t + 1],
             )
 
-            o = work.tile([P, QUAD, HID], F32, name="o", tag="o")
-            for pr in range(2):
-                m2 = ps_m2.tile([P, 2, HID], F32, name="m2", tag="m2")
-                for s in range(2):
-                    w0 = (2 * pr + s) * P
-                    nc.tensor.matmul_mx(
-                        out=m2[:, s, :],
-                        lhsT=c2[:, w0 : w0 + P].bitcast(FP8X4),
-                        lhsT_scale=s2[:, w0 : w0 + P],
-                        rhs=w1cod[:].bitcast(FP8X4),
-                        rhs_scale=w1sc[:],
-                        start=True,
-                        stop=True,
-                    )
-                nc.vector.tensor_tensor(
-                    out=o[:, 2 * pr : 2 * pr + 2, :],
-                    in0=m2[:],
-                    in1=b1bc[:].unsqueeze(1).to_broadcast([P, 2, HID]),
-                    op=ALU.add,
+        def regroup_scalar(q):
+            if not 0 <= q < NQ:
+                return
+            g2[q] = w2.tile([P, QUAD * P, 4], BF16, name="g2", tag="g2", align_bytes=64)
+            regroup(nc.scalar.copy, g2[q][:, RG_V:, :], planes[q][:, :, RG_V:])
+
+        def regroup_vector_quantise(q):
+            if not 0 <= q < NQ:
+                return
+            regroup(nc.vector.tensor_copy, g2[q][:, :RG_V, :], planes[q][:, :, :RG_V])
+            c2[q] = w2.tile([P, QUAD * P], U32, name="c2", tag="c2", align_bytes=64)
+            s2[q] = w2.tile([P, QUAD * P], U8, name="s2", tag="s2", align_bytes=64)
+            nc.vector.quantize_mx(
+                out=c2[q][:].bitcast(FP8X4),
+                scales=s2[q][:],
+                in_=g2[q][:].rearrange("p w t -> p (w t)"),
+            )
+
+        def mlp_matmul(j):
+            if not 0 <= j < NPAIR:
+                return
+            q = j // 2
+            m2[j] = ps_m2.tile([P, 2, HID], F32, name="m2", tag="m2")
+            for e in range(2):
+                w0 = (2 * (j % 2) + e) * P
+                nc.tensor.matmul_mx(
+                    out=m2[j][:, e, :],
+                    lhsT=c2[q][:, w0 : w0 + P].bitcast(FP8X4),
+                    lhsT_scale=s2[q][:, w0 : w0 + P],
+                    rhs=w1cod[:].bitcast(FP8X4),
+                    rhs_scale=w1sc[:],
+                    start=True,
+                    stop=True,
                 )
-            res = work.tile([P, QUAD, HID], F32, name="res", tag="res")
-            nc.scalar.activation(out=res[:], in_=o[:], func=ACT.Gelu_apprx_tanh)
+
+        def mlp_bias(j):
+            if not 0 <= j < NPAIR:
+                return
+            q = j // 2
+            if j % 2 == 0:
+                o[q] = w2.tile([P, QUAD, HID], F32, name="o", tag="o")
+            nc.vector.tensor_tensor(
+                out=o[q][:, 2 * (j % 2) : 2 * (j % 2) + 2, :],
+                in0=m2[j][:],
+                in1=b1bc[:].unsqueeze(1).to_broadcast([P, 2, HID]),
+                op=ALU.add,
+            )
+
+        def gelu_store(q):
+            if not 0 <= q < NQ:
+                return
+            res = w3.tile([P, QUAD, HID], F32, name="res", tag="res")
+            nc.scalar.activation(out=res[:], in_=o[q][:], func=ACT.Gelu_apprx_tanh)
             nc.sync.dma_start(out=out_v[:, q * QUAD : (q + 1) * QUAD, :], in_=res[:])
+
+        for j in range(-6, NPAIR + 7):
+            even = j % 2 == 0
+            if even and j >= 0:
+                load(j // 2 + LOAD_AHEAD)
+            squares(j - 1)
+            if even:
+                gain_bias((j - 4) // 2, 2)
+                gain_bias((j - 4) // 2, 3)
+                regroup_scalar((j - 4) // 2)
+            else:
+                gain_bias((j - 3) // 2, 0)
+                gain_bias((j - 3) // 2, 1)
+            h2_copy(j + 5)
+            normalise(j - 1)
+            mlp_matmul(j - 5)
+            feat_matmul(2 * j + 2)
+            feat_matmul(2 * j + 3)
+            pos_matmul(2 * j + 2)
+            pos_matmul(2 * j + 3)
+            if even:
+                z_transposes((j - 2) // 2, 0)
+                z_transposes((j - 2) // 2, 1)
+            else:
+                z_transposes((j - 3) // 2, 2)
+                z_transposes((j - 3) // 2, 3)
+            h2_transposes(j + 6)
+            residual(2 * j)
+            residual(2 * j + 1)
+            mlp_bias(j - 5)
+            if even:
+                regroup_vector_quantise((j - 4) // 2)
+                gelu_store((j - 6) // 2)
+            else:
+                h2_quantise((j + 3) // 2)
+            if j == 1:
+                quantise_w1()

@@ -18,8 +18,8 @@ NQ = B // QUAD
 NPAIR = B // 2
 EPS = 1e-5
 FLOPS = 2 * B * N * (D * D + N * D + D * HID)
-LOAD_AHEAD = 5
-RG_V = 384
+PAIR_W = 2 * P
+RG_V = 192
 
 
 def tile_gatblock_pb_t_kernel(
@@ -32,24 +32,21 @@ def tile_gatblock_pb_t_kernel(
 
     with ExitStack() as ctx:
         const = ctx.enter_context(tc.tile_pool(name="const", bufs=1))
-        xin = ctx.enter_context(tc.tile_pool(name="xin", bufs=LOAD_AHEAD + 1))
-        hin = ctx.enter_context(tc.tile_pool(name="hin", bufs=LOAD_AHEAD + 1))
-        xbp = ctx.enter_context(tc.tile_pool(name="xbp", bufs=3))
-        zp = ctx.enter_context(tc.tile_pool(name="zp", bufs=2))
+        xin = ctx.enter_context(tc.tile_pool(name="xin", bufs=4))
+        hin = ctx.enter_context(tc.tile_pool(name="hin", bufs=6))
+        w4 = ctx.enter_context(tc.tile_pool(name="w4", bufs=4))
         w3 = ctx.enter_context(tc.tile_pool(name="w3", bufs=3))
         w2 = ctx.enter_context(tc.tile_pool(name="w2", bufs=2))
-        stat = ctx.enter_context(tc.tile_pool(name="stat", bufs=4))
         ps_tr = ctx.enter_context(tc.psum_pool(name="ps_tr", bufs=3))
-        ps_mx = ctx.enter_context(tc.psum_pool(name="ps_mx", bufs=2))
+        ps_mm = ctx.enter_context(tc.psum_pool(name="ps_mm", bufs=3))
         ps_pos = ctx.enter_context(tc.psum_pool(name="ps_pos", bufs=2))
-        ps_m2 = ctx.enter_context(tc.psum_pool(name="ps_m2", bufs=1))
         ctx.enter_context(tc.manual_schedule())
 
         xq, hq, t1, g1, c1, s1 = {}, {}, {}, {}, {}, {}
         mx, pos, xb, sums, nm, ssq, rstd = {}, {}, {}, {}, {}, {}, {}
         z, zt, planes, g2, c2, s2, m2, o = {}, {}, {}, {}, {}, {}, {}, {}
 
-        def load(q):
+        def load_h(q):
             if not 0 <= q < NQ:
                 return
             hq[q] = hin.tile([P, QUAD * D], BF16, name="hq", tag="hq")
@@ -57,6 +54,10 @@ def tile_gatblock_pb_t_kernel(
                 out=hq[q][:].rearrange("p (s f) -> p s f", s=QUAD),
                 in_=h2_v[:, q * QUAD : (q + 1) * QUAD, :],
             )
+
+        def load_x(q):
+            if not 0 <= q < NQ:
+                return
             xq[q] = xin.tile([P, QUAD * D], BF16, name="xq", tag="xq")
             nc.sync.dma_start(
                 out=xq[q][:].rearrange("p (s f) -> p s f", s=QUAD),
@@ -81,12 +82,16 @@ def tile_gatblock_pb_t_kernel(
         nc.vector.memset(warm[:], 0.0)
         nc.scalar.activation(out=warm[:], in_=warm[:], func=ACT.Gelu_apprx_tanh)
 
-        load(0)
-        load(1)
+        load_h(0)
+        load_h(1)
+        load_h(2)
+        load_x(0)
+        load_h(3)
+        load_x(1)
         w1raw = const.tile([P, 4, HID], BF16, name="w1raw")
         nc.sync.dma_start(out=w1raw[:], in_=mlp_w1.rearrange("(t p) c -> p t c", p=P))
-        for q in range(2, LOAD_AHEAD):
-            load(q)
+        load_h(4)
+        load_x(2)
 
         ident_f = const.tile([P, P], F32, name="ident_f")
         make_identity(nc, ident_f[:])
@@ -141,41 +146,36 @@ def tile_gatblock_pb_t_kernel(
                 return
             h_w = hq[j // 2][:].bitcast(F32)
             t1[j] = ps_tr.tile([P, 2, 2, P], F32, name="t1", tag="tr")
-            for s in range(2):
+            for e in range(2):
                 for u in range(2):
-                    c0 = (2 * (j % 2) + s) * (D // 2) + u * P
-                    nc.tensor.transpose(t1[j][:, s, u, :], h_w[:, c0 : c0 + P], ident_f[:])
+                    c0 = (2 * (j % 2) + e) * (D // 2) + u * P
+                    nc.tensor.transpose(t1[j][:, e, u, :], h_w[:, c0 : c0 + P], ident_f[:])
 
         def h2_copy(j):
             if not 0 <= j < NPAIR:
                 return
-            q = j // 2
-            if j % 2 == 0:
-                g1[q] = w3.tile([P, QUAD * D], BF16, name="g1", tag="g1", align_bytes=64)
-            g1_w = g1[q][:].bitcast(F32)
+            g1[j] = w3.tile([P, 2 * D], BF16, name="g1", tag="g1", align_bytes=64)
             nc.scalar.copy(
-                out=g1_w[:, (j % 2) * D : (j % 2 + 1) * D].rearrange(
-                    "p (s n u) -> p s n u", s=2, u=2
-                ),
-                in_=t1[j][:].rearrange("p s u n -> p s n u"),
+                out=g1[j][:].bitcast(F32).rearrange("p (e n u) -> p e n u", e=2, u=2),
+                in_=t1[j][:].rearrange("p e u n -> p e n u"),
             )
 
-        def h2_quantise(q):
-            if not 0 <= q < NQ:
+        def h2_quantise(j):
+            if not 0 <= j < NPAIR:
                 return
-            c1[q] = w3.tile([P, QUAD * P], U32, name="c1", tag="c1", align_bytes=64)
-            s1[q] = w3.tile([P, QUAD * P], U8, name="s1", tag="s1", align_bytes=64)
-            nc.vector.quantize_mx(out=c1[q][:].bitcast(FP8X4), scales=s1[q][:], in_=g1[q][:])
+            c1[j] = w4.tile([P, PAIR_W], U32, name="c1", tag="c1", align_bytes=64)
+            s1[j] = w4.tile([P, PAIR_W], U8, name="s1", tag="s1", align_bytes=64)
+            nc.vector.quantize_mx(out=c1[j][:].bitcast(FP8X4), scales=s1[j][:], in_=g1[j][:])
 
         def feat_matmul(s):
             if not 0 <= s < B:
                 return
-            q, i = s // QUAD, s % QUAD
-            mx[s] = ps_mx.tile([P, D], F32, name="mx", tag="mx")
+            j, e = s // 2, s % 2
+            mx[s] = ps_mm.tile([P, D], F32, name="mx", tag="mm")
             nc.tensor.matmul_mx(
                 out=mx[s][:],
-                lhsT=c1[q][:, i * P : (i + 1) * P].bitcast(FP8X4),
-                lhsT_scale=s1[q][:, i * P : (i + 1) * P],
+                lhsT=c1[j][:, e * P : (e + 1) * P].bitcast(FP8X4),
+                lhsT_scale=s1[j][:, e * P : (e + 1) * P],
                 rhs=wcod[:].bitcast(FP8X4),
                 rhs_scale=wsc[:],
                 start=True,
@@ -187,21 +187,17 @@ def tile_gatblock_pb_t_kernel(
                 return
             q, i = s // QUAD, s % QUAD
             pos[s] = ps_pos.tile([P, D], F32, name="pos", tag="pos")
+            nc.tensor.matmul(
+                out=pos[s][:], lhsT=pmT[:], rhs=hq[q][:, i * D : (i + 1) * D], start=True, stop=False
+            )
             for c in range(4):
-                nc.tensor.matmul(
-                    out=pos[s][:, c * P : (c + 1) * P],
-                    lhsT=pmT[:],
-                    rhs=hq[q][:, i * D + c * P : i * D + (c + 1) * P],
-                    start=True,
-                    stop=False,
-                )
                 nc.tensor.matmul(
                     out=pos[s][:, c * P : (c + 1) * P],
                     lhsT=betacol[:, c, :],
                     rhs=ident_f[:],
                     is_transpose=True,
                     start=False,
-                    stop=True,
+                    stop=(c == 3),
                 )
 
         def residual(s):
@@ -209,9 +205,9 @@ def tile_gatblock_pb_t_kernel(
                 return
             q, i, j = s // QUAD, s % QUAD, s // 2
             if i == 0:
-                xb[q] = xbp.tile([P, QUAD, D], F32, name="xb", tag="xb")
+                xb[q] = w3.tile([P, QUAD, D], F32, name="xb", tag="xb")
             if s % 2 == 0:
-                sums[j] = stat.tile([P, 2], F32, name="sums", tag="sums")
+                sums[j] = w4.tile([P, 2], F32, name="sums", tag="sums")
             nc.vector.tensor_tensor(
                 out=xb[q][:, i, :], in0=mx[s][:], in1=xq[q][:, i * D : (i + 1) * D], op=ALU.add
             )
@@ -228,9 +224,9 @@ def tile_gatblock_pb_t_kernel(
         def squares(j):
             if not 0 <= j < NPAIR:
                 return
-            nm[j] = stat.tile([P, 2], F32, name="nm", tag="nm")
+            nm[j] = w4.tile([P, 2], F32, name="nm", tag="nm")
             nc.scalar.activation(out=nm[j][:], in_=sums[j][:], func=ACT.Copy, scale=-1.0 / D)
-            ssq[j] = stat.tile([P, 2], F32, name="ssq", tag="ssq")
+            ssq[j] = w4.tile([P, 2], F32, name="ssq", tag="ssq")
             for e in range(2):
                 s = 2 * j + e
                 junk = w2.tile([P, D], BF16, name="junk", tag="junk")
@@ -247,14 +243,14 @@ def tile_gatblock_pb_t_kernel(
             if not 0 <= j < NPAIR:
                 return
             q = j // 2
-            var = stat.tile([P, 2], F32, name="var", tag="var")
+            var = w4.tile([P, 2], F32, name="var", tag="var")
             nc.gpsimd.tensor_scalar(
                 out=var[:], in0=ssq[j][:], scalar1=1.0 / D, scalar2=EPS, op0=ALU.mult, op1=ALU.add
             )
-            rstd[j] = stat.tile([P, 2], F32, name="rstd", tag="rstd")
+            rstd[j] = w4.tile([P, 2], F32, name="rstd", tag="rstd")
             nc.gpsimd.tensor_tensor(out=rstd[j][:], in0=var[:], in1=mhalf[:], op=ALU.pow)
             if j % 2 == 0:
-                z[q] = zp.tile([P, QUAD, D], F32, name="z", tag="z")
+                z[q] = w3.tile([P, QUAD, D], F32, name="z", tag="z")
             for e in range(2):
                 i = 2 * (j % 2) + e
                 nc.gpsimd.tensor_scalar(
@@ -286,35 +282,37 @@ def tile_gatblock_pb_t_kernel(
                 scale=gT[:, t : t + 1],
             )
 
-        def regroup_scalar(q):
-            if not 0 <= q < NQ:
+        def regroup_scalar(j):
+            if not 0 <= j < NPAIR:
                 return
-            g2[q] = w2.tile([P, QUAD * P, 4], BF16, name="g2", tag="g2", align_bytes=64)
-            regroup(nc.scalar.copy, g2[q][:, RG_V:, :], planes[q][:, :, RG_V:])
+            w0 = (j % 2) * PAIR_W
+            g2[j] = w3.tile([P, PAIR_W, 4], BF16, name="g2", tag="g2", align_bytes=64)
+            regroup(
+                nc.scalar.copy, g2[j][:, RG_V:, :], planes[j // 2][:, :, w0 + RG_V : w0 + PAIR_W]
+            )
 
-        def regroup_vector_quantise(q):
-            if not 0 <= q < NQ:
+        def regroup_vector_quantise(j):
+            if not 0 <= j < NPAIR:
                 return
-            regroup(nc.vector.tensor_copy, g2[q][:, :RG_V, :], planes[q][:, :, :RG_V])
-            c2[q] = w2.tile([P, QUAD * P], U32, name="c2", tag="c2", align_bytes=64)
-            s2[q] = w2.tile([P, QUAD * P], U8, name="s2", tag="s2", align_bytes=64)
+            w0 = (j % 2) * PAIR_W
+            regroup(nc.vector.tensor_copy, g2[j][:, :RG_V, :], planes[j // 2][:, :, w0 : w0 + RG_V])
+            c2[j] = w3.tile([P, PAIR_W], U32, name="c2", tag="c2", align_bytes=64)
+            s2[j] = w3.tile([P, PAIR_W], U8, name="s2", tag="s2", align_bytes=64)
             nc.vector.quantize_mx(
-                out=c2[q][:].bitcast(FP8X4),
-                scales=s2[q][:],
-                in_=g2[q][:].rearrange("p w t -> p (w t)"),
+                out=c2[j][:].bitcast(FP8X4),
+                scales=s2[j][:],
+                in_=g2[j][:].rearrange("p w t -> p (w t)"),
             )
 
         def mlp_matmul(j):
             if not 0 <= j < NPAIR:
                 return
-            q = j // 2
-            m2[j] = ps_m2.tile([P, 2, HID], F32, name="m2", tag="m2")
+            m2[j] = ps_mm.tile([P, 2, HID], F32, name="m2", tag="mm")
             for e in range(2):
-                w0 = (2 * (j % 2) + e) * P
                 nc.tensor.matmul_mx(
                     out=m2[j][:, e, :],
-                    lhsT=c2[q][:, w0 : w0 + P].bitcast(FP8X4),
-                    lhsT_scale=s2[q][:, w0 : w0 + P],
+                    lhsT=c2[j][:, e * P : (e + 1) * P].bitcast(FP8X4),
+                    lhsT_scale=s2[j][:, e * P : (e + 1) * P],
                     rhs=w1cod[:].bitcast(FP8X4),
                     rhs_scale=w1sc[:],
                     start=True,
@@ -324,56 +322,44 @@ def tile_gatblock_pb_t_kernel(
         def mlp_bias(j):
             if not 0 <= j < NPAIR:
                 return
-            q = j // 2
-            if j % 2 == 0:
-                o[q] = w2.tile([P, QUAD, HID], F32, name="o", tag="o")
+            o[j] = w2.tile([P, 2, HID], F32, name="o", tag="o")
             nc.vector.tensor_tensor(
-                out=o[q][:, 2 * (j % 2) : 2 * (j % 2) + 2, :],
+                out=o[j][:],
                 in0=m2[j][:],
                 in1=b1bc[:].unsqueeze(1).to_broadcast([P, 2, HID]),
                 op=ALU.add,
             )
 
-        def gelu_store(q):
-            if not 0 <= q < NQ:
+        def gelu_store(j):
+            if not 0 <= j < NPAIR:
                 return
-            res = w3.tile([P, QUAD, HID], F32, name="res", tag="res")
-            nc.scalar.activation(out=res[:], in_=o[q][:], func=ACT.Gelu_apprx_tanh)
-            nc.sync.dma_start(out=out_v[:, q * QUAD : (q + 1) * QUAD, :], in_=res[:])
+            res = w3.tile([P, 2, HID], F32, name="res", tag="res")
+            nc.scalar.activation(out=res[:], in_=o[j][:], func=ACT.Gelu_apprx_tanh)
+            nc.sync.dma_start(out=out_v[:, 2 * j : 2 * j + 2, :], in_=res[:])
 
-        for j in range(-6, NPAIR + 7):
-            even = j % 2 == 0
-            if even and j >= 0:
-                load(j // 2 + LOAD_AHEAD)
+        for j in range(-4, NPAIR + 10):
+            if j >= 0 and j % 2 == 0:
+                load_h(j // 2 + 5)
+                load_x(j // 2 + 3)
+            gain_bias((j - 5) // 2, 2 * ((j - 5) % 2))
+            gain_bias((j - 5) // 2, 2 * ((j - 5) % 2) + 1)
+            h2_copy(j + 3)
             squares(j - 1)
-            if even:
-                gain_bias((j - 4) // 2, 2)
-                gain_bias((j - 4) // 2, 3)
-                regroup_scalar((j - 4) // 2)
-            else:
-                gain_bias((j - 3) // 2, 0)
-                gain_bias((j - 3) // 2, 1)
-            h2_copy(j + 5)
+            regroup_scalar(j - 6)
             normalise(j - 1)
-            mlp_matmul(j - 5)
             feat_matmul(2 * j + 2)
-            feat_matmul(2 * j + 3)
+            z_transposes((j - 4) // 2, 2 * ((j - 4) % 2))
             pos_matmul(2 * j + 2)
+            z_transposes((j - 4) // 2, 2 * ((j - 4) % 2) + 1)
+            h2_transposes(j + 4)
+            mlp_matmul(j - 8)
+            feat_matmul(2 * j + 3)
             pos_matmul(2 * j + 3)
-            if even:
-                z_transposes((j - 2) // 2, 0)
-                z_transposes((j - 2) // 2, 1)
-            else:
-                z_transposes((j - 3) // 2, 2)
-                z_transposes((j - 3) // 2, 3)
-            h2_transposes(j + 6)
             residual(2 * j)
+            mlp_bias(j - 9)
+            h2_quantise(j + 2)
             residual(2 * j + 1)
-            mlp_bias(j - 5)
-            if even:
-                regroup_vector_quantise((j - 4) // 2)
-                gelu_store((j - 6) // 2)
-            else:
-                h2_quantise((j + 3) // 2)
+            regroup_vector_quantise(j - 7)
             if j == 1:
                 quantise_w1()
+            gelu_store(j - 9)

@@ -43,7 +43,7 @@ def tile_gatblock_pb_t_kernel(
         ctx.enter_context(tc.manual_schedule())
 
         xq, hq, t1, g1, c1, s1 = {}, {}, {}, {}, {}, {}
-        mx, pos, xb, sums, nm, ssq, rstd = {}, {}, {}, {}, {}, {}, {}
+        mx, pos, xb, sums, nm, ssq, rstd, nmr = {}, {}, {}, {}, {}, {}, {}, {}
         z, zt, planes, g2, c2, s2, m2, o = {}, {}, {}, {}, {}, {}, {}, {}
 
         def load_h(q):
@@ -249,18 +249,35 @@ def tile_gatblock_pb_t_kernel(
             )
             rstd[j] = w4.tile([P, 2], F32, name="rstd", tag="rstd")
             nc.gpsimd.tensor_tensor(out=rstd[j][:], in0=var[:], in1=mhalf[:], op=ALU.pow)
+            nmr[j] = w4.tile([P, 2], F32, name="nmr", tag="nmr")
+            nc.gpsimd.tensor_tensor(out=nmr[j][:], in0=nm[j][:], in1=rstd[j][:], op=ALU.mult)
             if j % 2 == 0:
                 z[q] = w3.tile([P, QUAD, D], F32, name="z", tag="z")
-            for e in range(2):
-                i = 2 * (j % 2) + e
-                nc.gpsimd.tensor_scalar(
-                    out=z[q][:, i, :],
-                    in0=xb[q][:, i, :],
-                    scalar1=nm[j][:, e : e + 1],
-                    scalar2=rstd[j][:, e : e + 1],
-                    op0=ALU.add,
-                    op1=ALU.mult,
-                )
+
+        def centre_scale(eng, s):
+            if not 0 <= s < B:
+                return
+            q, i, j, e = s // QUAD, s % QUAD, s // 2, s % 2
+            eng.tensor_scalar(
+                out=z[q][:, i, :],
+                in0=xb[q][:, i, :],
+                scalar1=nm[j][:, e : e + 1],
+                scalar2=rstd[j][:, e : e + 1],
+                op0=ALU.add,
+                op1=ALU.mult,
+            )
+
+        def centre_scale_scalar(s):
+            if not 0 <= s < B:
+                return
+            q, i, j, e = s // QUAD, s % QUAD, s // 2, s % 2
+            nc.scalar.activation(
+                out=z[q][:, i, :],
+                in_=xb[q][:, i, :],
+                func=ACT.Identity,
+                bias=nmr[j][:, e : e + 1],
+                scale=rstd[j][:, e : e + 1],
+            )
 
         def z_transposes(q, t):
             if not 0 <= q < NQ:
@@ -346,7 +363,11 @@ def tile_gatblock_pb_t_kernel(
             h2_copy(j + 3)
             squares(j - 1)
             regroup_scalar(j - 6)
+            if j % 2 == 1:
+                centre_scale_scalar(2 * (j - 2) + 1)
             normalise(j - 1)
+            if j % 2 == 1:
+                centre_scale(nc.gpsimd, 2 * (j - 1))
             feat_matmul(2 * j + 2)
             z_transposes((j - 4) // 2, 2 * ((j - 4) % 2))
             pos_matmul(2 * j + 2)
@@ -359,6 +380,7 @@ def tile_gatblock_pb_t_kernel(
             mlp_bias(j - 9)
             h2_quantise(j + 2)
             residual(2 * j + 1)
+            centre_scale(nc.vector, 2 * (j - 2) + (j + 1) % 2)
             regroup_vector_quantise(j - 7)
             if j == 1:
                 quantise_w1()

@@ -40,10 +40,9 @@ def tile_gatblock_pb_t_kernel(
         ps_tr = ctx.enter_context(tc.psum_pool(name="ps_tr", bufs=3))
         ps_mm = ctx.enter_context(tc.psum_pool(name="ps_mm", bufs=3))
         ps_pos = ctx.enter_context(tc.psum_pool(name="ps_pos", bufs=2))
-        ctx.enter_context(tc.manual_schedule())
 
         xq, hq, t1, g1, c1, s1 = {}, {}, {}, {}, {}, {}
-        mx, pos, xb, sums, nm, ssq, rstd, nmr = {}, {}, {}, {}, {}, {}, {}, {}
+        mx, pos, xb, sums, nm, ssq, rstd = {}, {}, {}, {}, {}, {}, {}
         z, zt, planes, g2, c2, s2, m2, o = {}, {}, {}, {}, {}, {}, {}, {}
 
         def load_h(q):
@@ -249,35 +248,18 @@ def tile_gatblock_pb_t_kernel(
             )
             rstd[j] = w4.tile([P, 2], F32, name="rstd", tag="rstd")
             nc.gpsimd.tensor_tensor(out=rstd[j][:], in0=var[:], in1=mhalf[:], op=ALU.pow)
-            nmr[j] = w4.tile([P, 2], F32, name="nmr", tag="nmr")
-            nc.gpsimd.tensor_tensor(out=nmr[j][:], in0=nm[j][:], in1=rstd[j][:], op=ALU.mult)
             if j % 2 == 0:
                 z[q] = w3.tile([P, QUAD, D], F32, name="z", tag="z")
-
-        def centre_scale(eng, s):
-            if not 0 <= s < B:
-                return
-            q, i, j, e = s // QUAD, s % QUAD, s // 2, s % 2
-            eng.tensor_scalar(
-                out=z[q][:, i, :],
-                in0=xb[q][:, i, :],
-                scalar1=nm[j][:, e : e + 1],
-                scalar2=rstd[j][:, e : e + 1],
-                op0=ALU.add,
-                op1=ALU.mult,
-            )
-
-        def centre_scale_scalar(s):
-            if not 0 <= s < B:
-                return
-            q, i, j, e = s // QUAD, s % QUAD, s // 2, s % 2
-            nc.scalar.activation(
-                out=z[q][:, i, :],
-                in_=xb[q][:, i, :],
-                func=ACT.Identity,
-                bias=nmr[j][:, e : e + 1],
-                scale=rstd[j][:, e : e + 1],
-            )
+            for e in range(2):
+                i = 2 * (j % 2) + e
+                nc.gpsimd.tensor_scalar(
+                    out=z[q][:, i, :],
+                    in0=xb[q][:, i, :],
+                    scalar1=nm[j][:, e : e + 1],
+                    scalar2=rstd[j][:, e : e + 1],
+                    op0=ALU.add,
+                    op1=ALU.mult,
+                )
 
         def z_transposes(q, t):
             if not 0 <= q < NQ:
@@ -363,11 +345,7 @@ def tile_gatblock_pb_t_kernel(
             h2_copy(j + 3)
             squares(j - 1)
             regroup_scalar(j - 6)
-            if j % 2 == 1:
-                centre_scale_scalar(2 * (j - 2) + 1)
             normalise(j - 1)
-            if j % 2 == 1:
-                centre_scale(nc.gpsimd, 2 * (j - 1))
             feat_matmul(2 * j + 2)
             z_transposes((j - 4) // 2, 2 * ((j - 4) % 2))
             pos_matmul(2 * j + 2)
@@ -380,7 +358,6 @@ def tile_gatblock_pb_t_kernel(
             mlp_bias(j - 9)
             h2_quantise(j + 2)
             residual(2 * j + 1)
-            centre_scale(nc.vector, 2 * (j - 2) + (j + 1) % 2)
             regroup_vector_quantise(j - 7)
             if j == 1:
                 quantise_w1()

@@ -20,6 +20,7 @@ EPS = 1e-5
 FLOPS = 2 * B * N * (D * D + N * D + D * HID)
 PAIR_W = 2 * P
 RG_V = 192
+GP_BIAS = (3,)
 
 
 def tile_gatblock_pb_t_kernel(
@@ -42,7 +43,7 @@ def tile_gatblock_pb_t_kernel(
         ps_pos = ctx.enter_context(tc.psum_pool(name="ps_pos", bufs=2))
 
         xq, hq, t1, g1, c1, s1 = {}, {}, {}, {}, {}, {}
-        mx, pos, xb, sums, nm, ssq, rstd = {}, {}, {}, {}, {}, {}, {}
+        mx, pos, xb, sums, nm, ssq, rstd, xbeta = {}, {}, {}, {}, {}, {}, {}, {}
         z, zt, planes, g2, c2, s2, m2, o = {}, {}, {}, {}, {}, {}, {}, {}
 
         def load_h(q):
@@ -75,6 +76,8 @@ def tile_gatblock_pb_t_kernel(
         nc.scalar.dma_start(out=gbrow[0:4, :], in_=ln2_g.rearrange("(t p) -> t p", p=P))
         nc.scalar.dma_start(out=gbrow[4:8, :], in_=ln2_b.rearrange("(t p) -> t p", p=P))
         nc.scalar.dma_start(out=gbrow[8:12, :], in_=xfeat_b.rearrange("(t p) -> t p", p=P))
+        betabc = const.tile([P, D], BF16, name="betabc")
+        nc.scalar.dma_start(out=betabc[:], in_=xfeat_b.partition_broadcast(P))
         b1bc = const.tile([P, HID], BF16, name="b1bc")
         nc.scalar.dma_start(out=b1bc[:], in_=mlp_b1.partition_broadcast(P))
         warm = const.tile([P, 1], F32, name="warm")
@@ -187,9 +190,13 @@ def tile_gatblock_pb_t_kernel(
             q, i = s // QUAD, s % QUAD
             pos[s] = ps_pos.tile([P, D], F32, name="pos", tag="pos")
             nc.tensor.matmul(
-                out=pos[s][:], lhsT=pmT[:], rhs=hq[q][:, i * D : (i + 1) * D], start=True, stop=False
+                out=pos[s][:],
+                lhsT=pmT[:],
+                rhs=hq[q][:, i * D : (i + 1) * D],
+                start=True,
+                stop=(i in GP_BIAS),
             )
-            for c in range(4):
+            for c in range(0 if i in GP_BIAS else 4):
                 nc.tensor.matmul(
                     out=pos[s][:, c * P : (c + 1) * P],
                     lhsT=betacol[:, c, :],
@@ -198,6 +205,15 @@ def tile_gatblock_pb_t_kernel(
                     start=False,
                     stop=(c == 3),
                 )
+
+        def bias_gpsimd(s):
+            if not 0 <= s < B or s % QUAD not in GP_BIAS:
+                return
+            q, i = s // QUAD, s % QUAD
+            xbeta[s] = w3.tile([P, D], F32, name="xbeta", tag="xbeta")
+            nc.gpsimd.tensor_tensor(
+                out=xbeta[s][:], in0=xq[q][:, i * D : (i + 1) * D], in1=betabc[:], op=ALU.add
+            )
 
         def residual(s):
             if not 0 <= s < B:
@@ -208,7 +224,10 @@ def tile_gatblock_pb_t_kernel(
             if s % 2 == 0:
                 sums[j] = w4.tile([P, 2], F32, name="sums", tag="sums")
             nc.vector.tensor_tensor(
-                out=xb[q][:, i, :], in0=mx[s][:], in1=xq[q][:, i * D : (i + 1) * D], op=ALU.add
+                out=xb[q][:, i, :],
+                in0=mx[s][:],
+                in1=xbeta[s][:] if i in GP_BIAS else xq[q][:, i * D : (i + 1) * D],
+                op=ALU.add,
             )
             nc.vector.scalar_tensor_tensor(
                 out=xb[q][:, i, :],
@@ -346,6 +365,8 @@ def tile_gatblock_pb_t_kernel(
             squares(j - 1)
             regroup_scalar(j - 6)
             normalise(j - 1)
+            bias_gpsimd(2 * j + 4)
+            bias_gpsimd(2 * j + 5)
             feat_matmul(2 * j + 2)
             z_transposes((j - 4) // 2, 2 * ((j - 4) % 2))
             pos_matmul(2 * j + 2)

@@ -19,8 +19,7 @@ NPAIR = B // 2
 EPS = 1e-5
 FLOPS = 2 * B * N * (D * D + N * D + D * HID)
 PAIR_W = 2 * P
-RG_V = 192
-GP_BIAS = (3,)
+RG_V = 128
 
 
 def tile_gatblock_pb_t_kernel(
@@ -43,7 +42,7 @@ def tile_gatblock_pb_t_kernel(
         ps_pos = ctx.enter_context(tc.psum_pool(name="ps_pos", bufs=2))
 
         xq, hq, t1, g1, c1, s1 = {}, {}, {}, {}, {}, {}
-        mx, pos, xb, sums, nm, ssq, rstd, xbeta = {}, {}, {}, {}, {}, {}, {}, {}
+        mx, pos, xb, sums, nm, ssq, rstd = {}, {}, {}, {}, {}, {}, {}
         z, zt, planes, g2, c2, s2, m2, o = {}, {}, {}, {}, {}, {}, {}, {}
 
         def load_h(q):
@@ -76,8 +75,6 @@ def tile_gatblock_pb_t_kernel(
         nc.scalar.dma_start(out=gbrow[0:4, :], in_=ln2_g.rearrange("(t p) -> t p", p=P))
         nc.scalar.dma_start(out=gbrow[4:8, :], in_=ln2_b.rearrange("(t p) -> t p", p=P))
         nc.scalar.dma_start(out=gbrow[8:12, :], in_=xfeat_b.rearrange("(t p) -> t p", p=P))
-        betabc = const.tile([P, D], BF16, name="betabc")
-        nc.scalar.dma_start(out=betabc[:], in_=xfeat_b.partition_broadcast(P))
         b1bc = const.tile([P, HID], BF16, name="b1bc")
         nc.scalar.dma_start(out=b1bc[:], in_=mlp_b1.partition_broadcast(P))
         warm = const.tile([P, 1], F32, name="warm")
@@ -190,13 +187,9 @@ def tile_gatblock_pb_t_kernel(
             q, i = s // QUAD, s % QUAD
             pos[s] = ps_pos.tile([P, D], F32, name="pos", tag="pos")
             nc.tensor.matmul(
-                out=pos[s][:],
-                lhsT=pmT[:],
-                rhs=hq[q][:, i * D : (i + 1) * D],
-                start=True,
-                stop=(i in GP_BIAS),
+                out=pos[s][:], lhsT=pmT[:], rhs=hq[q][:, i * D : (i + 1) * D], start=True, stop=False
             )
-            for c in range(0 if i in GP_BIAS else 4):
+            for c in range(4):
                 nc.tensor.matmul(
                     out=pos[s][:, c * P : (c + 1) * P],
                     lhsT=betacol[:, c, :],
@@ -205,15 +198,6 @@ def tile_gatblock_pb_t_kernel(
                     start=False,
                     stop=(c == 3),
                 )
-
-        def bias_gpsimd(s):
-            if not 0 <= s < B or s % QUAD not in GP_BIAS:
-                return
-            q, i = s // QUAD, s % QUAD
-            xbeta[s] = w3.tile([P, D], F32, name="xbeta", tag="xbeta")
-            nc.gpsimd.tensor_tensor(
-                out=xbeta[s][:], in0=xq[q][:, i * D : (i + 1) * D], in1=betabc[:], op=ALU.add
-            )
 
         def residual(s):
             if not 0 <= s < B:
@@ -224,10 +208,7 @@ def tile_gatblock_pb_t_kernel(
             if s % 2 == 0:
                 sums[j] = w4.tile([P, 2], F32, name="sums", tag="sums")
             nc.vector.tensor_tensor(
-                out=xb[q][:, i, :],
-                in0=mx[s][:],
-                in1=xbeta[s][:] if i in GP_BIAS else xq[q][:, i * D : (i + 1) * D],
-                op=ALU.add,
+                out=xb[q][:, i, :], in0=mx[s][:], in1=xq[q][:, i * D : (i + 1) * D], op=ALU.add
             )
             nc.vector.scalar_tensor_tensor(
                 out=xb[q][:, i, :],
@@ -365,8 +346,6 @@ def tile_gatblock_pb_t_kernel(
             squares(j - 1)
             regroup_scalar(j - 6)
             normalise(j - 1)
-            bias_gpsimd(2 * j + 4)
-            bias_gpsimd(2 * j + 5)
             feat_matmul(2 * j + 2)
             z_transposes((j - 4) // 2, 2 * ((j - 4) % 2))
             pos_matmul(2 * j + 2)

@@ -199,17 +199,22 @@ def tile_gatblock_pb_t_kernel(
                     stop=(c == 3),
                 )
 
-        def residual(s):
+        def add_x(s):
             if not 0 <= s < B:
                 return
-            q, i, j = s // QUAD, s % QUAD, s // 2
+            q, i = s // QUAD, s % QUAD
             if i == 0:
                 xb[q] = w3.tile([P, QUAD, D], F32, name="xb", tag="xb")
-            if s % 2 == 0:
-                sums[j] = w4.tile([P, 2], F32, name="sums", tag="sums")
             nc.vector.tensor_tensor(
                 out=xb[q][:, i, :], in0=mx[s][:], in1=xq[q][:, i * D : (i + 1) * D], op=ALU.add
             )
+
+        def add_pos(s):
+            if not 0 <= s < B:
+                return
+            q, i, j = s // QUAD, s % QUAD, s // 2
+            if s % 2 == 0:
+                sums[j] = w4.tile([P, 2], F32, name="sums", tag="sums")
             nc.vector.scalar_tensor_tensor(
                 out=xb[q][:, i, :],
                 in0=pos[s][:],
@@ -220,11 +225,15 @@ def tile_gatblock_pb_t_kernel(
                 accum_out=sums[j][:, s % 2 : s % 2 + 1],
             )
 
-        def squares(j):
+        def minus_mean(j):
             if not 0 <= j < NPAIR:
                 return
             nm[j] = w4.tile([P, 2], F32, name="nm", tag="nm")
             nc.scalar.activation(out=nm[j][:], in_=sums[j][:], func=ACT.Copy, scale=-1.0 / D)
+
+        def squares(j):
+            if not 0 <= j < NPAIR:
+                return
             ssq[j] = w4.tile([P, 2], F32, name="ssq", tag="ssq")
             for e in range(2):
                 s = 2 * j + e
@@ -290,11 +299,15 @@ def tile_gatblock_pb_t_kernel(
                 nc.scalar.copy, g2[j][:, RG_V:, :], planes[j // 2][:, :, w0 + RG_V : w0 + PAIR_W]
             )
 
-        def regroup_vector_quantise(j):
+        def regroup_vector(j):
             if not 0 <= j < NPAIR:
                 return
             w0 = (j % 2) * PAIR_W
             regroup(nc.vector.tensor_copy, g2[j][:, :RG_V, :], planes[j // 2][:, :, w0 : w0 + RG_V])
+
+        def h_quantise(j):
+            if not 0 <= j < NPAIR:
+                return
             c2[j] = w3.tile([P, PAIR_W], U32, name="c2", tag="c2", align_bytes=64)
             s2[j] = w3.tile([P, PAIR_W], U8, name="s2", tag="s2", align_bytes=64)
             nc.vector.quantize_mx(
@@ -340,6 +353,7 @@ def tile_gatblock_pb_t_kernel(
             if j >= 0 and j % 2 == 0:
                 load_h(j // 2 + 5)
                 load_x(j // 2 + 3)
+            minus_mean(j - 1)
             gain_bias((j - 5) // 2, 2 * ((j - 5) % 2))
             gain_bias((j - 5) // 2, 2 * ((j - 5) % 2) + 1)
             h2_copy(j + 3)
@@ -354,11 +368,14 @@ def tile_gatblock_pb_t_kernel(
             mlp_matmul(j - 8)
             feat_matmul(2 * j + 3)
             pos_matmul(2 * j + 3)
-            residual(2 * j)
+            add_x(2 * j)
+            add_x(2 * j + 1)
+            add_pos(2 * j)
+            add_pos(2 * j + 1)
+            regroup_vector(j - 7)
             mlp_bias(j - 9)
+            h_quantise(j - 7)
             h2_quantise(j + 2)
-            residual(2 * j + 1)
-            regroup_vector_quantise(j - 7)
             if j == 1:
                 quantise_w1()
             gelu_store(j - 9)

@@ -349,33 +349,34 @@ def tile_gatblock_pb_t_kernel(
             nc.scalar.activation(out=res[:], in_=o[j][:], func=ACT.Gelu_apprx_tanh)
             nc.sync.dma_start(out=out_v[:, 2 * j : 2 * j + 2, :], in_=res[:])
 
-        for j in range(-4, NPAIR + 10):
+        ctx.enter_context(tc.manual_schedule(engines={mybir.EngineType.PE, mybir.EngineType.DVE, mybir.EngineType.Activation, mybir.EngineType.Pool}))
+        for j in range(-4, NPAIR + 11):
             if j >= 0 and j % 2 == 0:
                 load_h(j // 2 + 5)
                 load_x(j // 2 + 3)
-            minus_mean(j - 1)
-            gain_bias((j - 5) // 2, 2 * ((j - 5) % 2))
-            gain_bias((j - 5) // 2, 2 * ((j - 5) % 2) + 1)
-            h2_copy(j + 3)
-            squares(j - 1)
-            regroup_scalar(j - 6)
-            normalise(j - 1)
+            mlp_matmul(j - 8)
             feat_matmul(2 * j + 2)
+            feat_matmul(2 * j + 3)
             z_transposes((j - 4) // 2, 2 * ((j - 4) % 2))
-            pos_matmul(2 * j + 2)
             z_transposes((j - 4) // 2, 2 * ((j - 4) % 2) + 1)
             h2_transposes(j + 4)
-            mlp_matmul(j - 8)
-            feat_matmul(2 * j + 3)
+            pos_matmul(2 * j + 2)
             pos_matmul(2 * j + 3)
             add_x(2 * j)
             add_x(2 * j + 1)
             add_pos(2 * j)
             add_pos(2 * j + 1)
-            regroup_vector(j - 7)
             mlp_bias(j - 9)
-            h_quantise(j - 7)
+            regroup_vector(j - 7)
             h2_quantise(j + 2)
+            h_quantise(j - 7)
             if j == 1:
                 quantise_w1()
-            gelu_store(j - 9)
+            minus_mean(j - 1)
+            gain_bias((j - 5) // 2, 2 * ((j - 5) % 2))
+            gain_bias((j - 5) // 2, 2 * ((j - 5) % 2) + 1)
+            h2_copy(j + 3)
+            gelu_store(j - 10)
+            regroup_scalar(j - 6)
+            squares(j - 1)
+            normalise(j - 1)

@@ -75,6 +75,14 @@ def tile_gatblock_pb_t_kernel(
         nc.scalar.dma_start(out=gbrow[0:4, :], in_=ln2_g.rearrange("(t p) -> t p", p=P))
         nc.scalar.dma_start(out=gbrow[4:8, :], in_=ln2_b.rearrange("(t p) -> t p", p=P))
         nc.scalar.dma_start(out=gbrow[8:12, :], in_=xfeat_b.rearrange("(t p) -> t p", p=P))
+        ones_row = const.tile([P, P], BF16, name="ones_row")
+        nc.vector.memset(ones_row[:], 0.0)
+        nc.vector.memset(ones_row[0:1, :], 1.0)
+        beta_row = const.tile([P, 2 * P], BF16, name="beta_row")
+        nc.vector.memset(beta_row[:], 0.0)
+        nc.scalar.dma_start(
+            out=beta_row[0:1, :], in_=xfeat_b[0 : 2 * P].rearrange("(o f) -> o f", o=1)
+        )
         b1bc = const.tile([P, HID], BF16, name="b1bc")
         nc.scalar.dma_start(out=b1bc[:], in_=mlp_b1.partition_broadcast(P))
         warm = const.tile([P, 1], F32, name="warm")
@@ -189,7 +197,15 @@ def tile_gatblock_pb_t_kernel(
             nc.tensor.matmul(
                 out=pos[s][:], lhsT=pmT[:], rhs=hq[q][:, i * D : (i + 1) * D], start=True, stop=False
             )
-            for c in range(4):
+            n_mm = 2 - s % 2
+            nc.tensor.matmul(
+                out=pos[s][:, : n_mm * P],
+                lhsT=ones_row[:],
+                rhs=beta_row[:, : n_mm * P],
+                start=False,
+                stop=False,
+            )
+            for c in range(n_mm, 4):
                 nc.tensor.matmul(
                     out=pos[s][:, c * P : (c + 1) * P],
                     lhsT=betacol[:, c, :],
@@ -357,10 +373,10 @@ def tile_gatblock_pb_t_kernel(
             mlp_matmul(j - 8)
             feat_matmul(2 * j + 2)
             feat_matmul(2 * j + 3)
-            z_transposes((j - 4) // 2, 2 * ((j - 4) % 2))
-            z_transposes((j - 4) // 2, 2 * ((j - 4) % 2) + 1)
             h2_transposes(j + 4)
             pos_matmul(2 * j + 2)
+            z_transposes((j - 4) // 2, 2 * ((j - 4) % 2))
+            z_transposes((j - 4) // 2, 2 * ((j - 4) % 2) + 1)
             pos_matmul(2 * j + 3)
             add_x(2 * j)
             add_x(2 * j + 1)

@@ -366,23 +366,23 @@ def tile_gatblock_pb_t_kernel(
             nc.sync.dma_start(out=out_v[:, 2 * j : 2 * j + 2, :], in_=res[:])
 
         ctx.enter_context(tc.manual_schedule(engines={mybir.EngineType.PE, mybir.EngineType.DVE, mybir.EngineType.Activation, mybir.EngineType.Pool}))
-        for j in range(-4, NPAIR + 11):
+        for j in range(-4, NPAIR + 10):
             if j >= 0 and j % 2 == 0:
                 load_h(j // 2 + 5)
                 load_x(j // 2 + 3)
             mlp_matmul(j - 8)
             feat_matmul(2 * j + 2)
             feat_matmul(2 * j + 3)
-            h2_transposes(j + 4)
-            pos_matmul(2 * j + 2)
             z_transposes((j - 4) // 2, 2 * ((j - 4) % 2))
             z_transposes((j - 4) // 2, 2 * ((j - 4) % 2) + 1)
+            h2_transposes(j + 4)
+            pos_matmul(2 * j + 2)
             pos_matmul(2 * j + 3)
+            mlp_bias(j - 9)
             add_x(2 * j)
             add_x(2 * j + 1)
             add_pos(2 * j)
             add_pos(2 * j + 1)
-            mlp_bias(j - 9)
             regroup_vector(j - 7)
             h2_quantise(j + 2)
             h_quantise(j - 7)
@@ -392,7 +392,7 @@ def tile_gatblock_pb_t_kernel(
             gain_bias((j - 5) // 2, 2 * ((j - 5) % 2))
             gain_bias((j - 5) // 2, 2 * ((j - 5) % 2) + 1)
             h2_copy(j + 3)
-            gelu_store(j - 10)
+            gelu_store(j - 9)
             regroup_scalar(j - 6)
             squares(j - 1)
             normalise(j - 1)

@@ -19,7 +19,7 @@ NPAIR = B // 2
 EPS = 1e-5
 FLOPS = 2 * B * N * (D * D + N * D + D * HID)
 PAIR_W = 2 * P
-RG_V = 128
+RG_V = 160
 
 
 def tile_gatblock_pb_t_kernel(
@@ -378,12 +378,12 @@ def tile_gatblock_pb_t_kernel(
             h2_transposes(j + 4)
             pos_matmul(2 * j + 2)
             pos_matmul(2 * j + 3)
+            regroup_vector(j - 7)
             mlp_bias(j - 9)
             add_x(2 * j)
             add_x(2 * j + 1)
             add_pos(2 * j)
             add_pos(2 * j + 1)
-            regroup_vector(j - 7)
             h2_quantise(j + 2)
             h_quantise(j - 7)
             if j == 1:
@@ -392,7 +392,7 @@ def tile_gatblock_pb_t_kernel(
             gain_bias((j - 5) // 2, 2 * ((j - 5) % 2))
             gain_bias((j - 5) // 2, 2 * ((j - 5) % 2) + 1)
             h2_copy(j + 3)
+            squares(j - 1)
             gelu_store(j - 9)
             regroup_scalar(j - 6)
-            squares(j - 1)
             normalise(j - 1)

from contextlib import ExitStack

import concourse.mybir as mybir
from concourse.masks import make_identity

F32 = mybir.dt.float32
BF16 = mybir.dt.bfloat16
U32 = mybir.dt.uint32
U8 = mybir.dt.uint8
FP8X4 = mybir.dt.float8_e4m3fn_x4
ALU = mybir.AluOpType
ACT = mybir.ActivationFunctionType

B, N, D, HID = 48, 128, 512, 256
P = 128
QUAD = 4
NQ = B // QUAD
NPAIR = B // 2
EPS = 1e-5
FLOPS = 2 * B * N * (D * D + N * D + D * HID)
PAIR_W = 2 * P
RG_V = 160


def tile_gatblock_pb_t_kernel(
    tc, x, h2, xfeat_w, xfeat_b, pos_mix, ln2_g, ln2_b, mlp_w1, mlp_b1, out
):
    nc = tc.nc
    x_v = x.rearrange("b n f -> n b f")
    h2_v = h2.rearrange("b n f -> n b f")
    out_v = out.rearrange("b n j -> n b j")

    with ExitStack() as ctx:
        const = ctx.enter_context(tc.tile_pool(name="const", bufs=1))
        xin = ctx.enter_context(tc.tile_pool(name="xin", bufs=4))
        hin = ctx.enter_context(tc.tile_pool(name="hin", bufs=6))
        w4 = ctx.enter_context(tc.tile_pool(name="w4", bufs=4))
        w3 = ctx.enter_context(tc.tile_pool(name="w3", bufs=3))
        w2 = ctx.enter_context(tc.tile_pool(name="w2", bufs=2))
        ps_tr = ctx.enter_context(tc.psum_pool(name="ps_tr", bufs=3))
        ps_mm = ctx.enter_context(tc.psum_pool(name="ps_mm", bufs=3))
        ps_pos = ctx.enter_context(tc.psum_pool(name="ps_pos", bufs=2))

        xq, hq, t1, g1, c1, s1 = {}, {}, {}, {}, {}, {}
        mx, pos, xb, sums, nm, ssq, rstd = {}, {}, {}, {}, {}, {}, {}
        z, zt, planes, g2, c2, s2, m2, o = {}, {}, {}, {}, {}, {}, {}, {}

        def load_h(q):
            if not 0 <= q < NQ:
                return
            hq[q] = hin.tile([P, QUAD * D], BF16, name="hq", tag="hq")
            nc.sync.dma_start(
                out=hq[q][:].rearrange("p (s f) -> p s f", s=QUAD),
                in_=h2_v[:, q * QUAD : (q + 1) * QUAD, :],
            )

        def load_x(q):
            if not 0 <= q < NQ:
                return
            xq[q] = xin.tile([P, QUAD * D], BF16, name="xq", tag="xq")
            nc.sync.dma_start(
                out=xq[q][:].rearrange("p (s f) -> p s f", s=QUAD),
                in_=x_v[:, q * QUAD : (q + 1) * QUAD, :],
            )

        wraw = const.tile([P, 4, D], BF16, name="wraw")
        nc.sync.dma_start(
            out=wraw[:].rearrange("p (u e) c -> p u (e c)", u=2),
            in_=xfeat_w.rearrange("(u p e) c -> p u (e c)", u=2, e=2),
        )
        pm = const.tile([P, P], BF16, name="pm")
        nc.scalar.dma_start(out=pm[:], in_=pos_mix)
        gbrow = const.tile([P, P], BF16, name="gbrow")
        nc.vector.memset(gbrow[:], 0.0)
        nc.scalar.dma_start(out=gbrow[0:4, :], in_=ln2_g.rearrange("(t p) -> t p", p=P))
        nc.scalar.dma_start(out=gbrow[4:8, :], in_=ln2_b.rearrange("(t p) -> t p", p=P))
        nc.scalar.dma_start(out=gbrow[8:12, :], in_=xfeat_b.rearrange("(t p) -> t p", p=P))
        ones_row = const.tile([P, P], BF16, name="ones_row")
        nc.vector.memset(ones_row[:], 0.0)
        nc.vector.memset(ones_row[0:1, :], 1.0)
        beta_row = const.tile([P, 2 * P], BF16, name="beta_row")
        nc.vector.memset(beta_row[:], 0.0)
        nc.scalar.dma_start(
            out=beta_row[0:1, :], in_=xfeat_b[0 : 2 * P].rearrange("(o f) -> o f", o=1)
        )
        b1bc = const.tile([P, HID], BF16, name="b1bc")
        nc.scalar.dma_start(out=b1bc[:], in_=mlp_b1.partition_broadcast(P))
        warm = const.tile([P, 1], F32, name="warm")
        nc.vector.memset(warm[:], 0.0)
        nc.scalar.activation(out=warm[:], in_=warm[:], func=ACT.Gelu_apprx_tanh)

        load_h(0)
        load_h(1)
        load_h(2)
        load_x(0)
        load_h(3)
        load_x(1)
        w1raw = const.tile([P, 4, HID], BF16, name="w1raw")
        nc.sync.dma_start(out=w1raw[:], in_=mlp_w1.rearrange("(t p) c -> p t c", p=P))
        load_h(4)
        load_x(2)

        ident_f = const.tile([P, P], F32, name="ident_f")
        make_identity(nc, ident_f[:])
        ident_b = const.tile([P, P], BF16, name="ident_b")
        make_identity(nc, ident_b[:])
        mhalf = const.tile([P, 2], F32, name="mhalf")
        nc.vector.memset(mhalf[:], -0.5)

        def regroup(eng_copy, dst, src):
            eng_copy(
                out=dst.rearrange("p (c i) t -> p c t i", i=4),
                in_=src.rearrange("p t (c i) -> p c t i", i=4),
            )

        wgrp = const.tile([P, D, 4], BF16, name="wgrp", align_bytes=64)
        regroup(nc.vector.tensor_copy, wgrp[:], wraw[:])
        wcod = const.tile([P, D], U32, name="wcod", align_bytes=64)
        wsc = const.tile([P, D], U8, name="wsc", align_bytes=64)
        nc.vector.quantize_mx(
            out=wcod[:].bitcast(FP8X4), scales=wsc[:], in_=wgrp[:].rearrange("p c t -> p (c t)")
        )

        pmT_ps = ps_tr.tile([P, P], BF16, name="pmT_ps", tag="tr")
        nc.tensor.transpose(pmT_ps[:], pm[:], ident_b[:])
        pmT = const.tile([P, P], BF16, name="pmT")
        nc.vector.tensor_copy(out=pmT[:], in_=pmT_ps[:])
        gb_ps = ps_tr.tile([P, P], BF16, name="gb_ps", tag="tr")
        nc.tensor.transpose(gb_ps[:], gbrow[:], ident_b[:])
        gT = const.tile([P, 4], F32, name="gT")
        nc.vector.tensor_copy(out=gT[:], in_=gb_ps[:, 0:4])
        bT = const.tile([P, 4], F32, name="bT")
        nc.vector.tensor_copy(out=bT[:], in_=gb_ps[:, 4:8])
        betacol = const.tile([P, 4, P], F32, name="betacol")
        nc.vector.tensor_copy(
            out=betacol[:], in_=gb_ps[:, 8:12].unsqueeze(2).to_broadcast([P, 4, P])
        )

        w1cod = const.tile([P, HID], U32, name="w1cod", align_bytes=64)
        w1sc = const.tile([P, HID], U8, name="w1sc", align_bytes=64)

        def quantise_w1():
            w1grp = const.tile([P, HID, 4], BF16, name="w1grp", align_bytes=64)
            regroup(nc.vector.tensor_copy, w1grp[:], w1raw[:])
            nc.vector.quantize_mx(
                out=w1cod[:].bitcast(FP8X4),
                scales=w1sc[:],
                in_=w1grp[:].rearrange("p c t -> p (c t)"),
            )

        def h2_transposes(j):
            if not 0 <= j < NPAIR:
                return
            h_w = hq[j // 2][:].bitcast(F32)
            t1[j] = ps_tr.tile([P, 2, 2, P], F32, name="t1", tag="tr")
            for e in range(2):
                for u in range(2):
                    c0 = (2 * (j % 2) + e) * (D // 2) + u * P
                    nc.tensor.transpose(t1[j][:, e, u, :], h_w[:, c0 : c0 + P], ident_f[:])

        def h2_copy(j):
            if not 0 <= j < NPAIR:
                return
            g1[j] = w3.tile([P, 2 * D], BF16, name="g1", tag="g1", align_bytes=64)
            nc.scalar.copy(
                out=g1[j][:].bitcast(F32).rearrange("p (e n u) -> p e n u", e=2, u=2),
                in_=t1[j][:].rearrange("p e u n -> p e n u"),
            )

        def h2_quantise(j):
            if not 0 <= j < NPAIR:
                return
            c1[j] = w4.tile([P, PAIR_W], U32, name="c1", tag="c1", align_bytes=64)
            s1[j] = w4.tile([P, PAIR_W], U8, name="s1", tag="s1", align_bytes=64)
            nc.vector.quantize_mx(out=c1[j][:].bitcast(FP8X4), scales=s1[j][:], in_=g1[j][:])

        def feat_matmul(s):
            if not 0 <= s < B:
                return
            j, e = s // 2, s % 2
            mx[s] = ps_mm.tile([P, D], F32, name="mx", tag="mm")
            nc.tensor.matmul_mx(
                out=mx[s][:],
                lhsT=c1[j][:, e * P : (e + 1) * P].bitcast(FP8X4),
                lhsT_scale=s1[j][:, e * P : (e + 1) * P],
                rhs=wcod[:].bitcast(FP8X4),
                rhs_scale=wsc[:],
                start=True,
                stop=True,
            )

        def pos_matmul(s):
            if not 0 <= s < B:
                return
            q, i = s // QUAD, s % QUAD
            pos[s] = ps_pos.tile([P, D], F32, name="pos", tag="pos")
            nc.tensor.matmul(
                out=pos[s][:], lhsT=pmT[:], rhs=hq[q][:, i * D : (i + 1) * D], start=True, stop=False
            )
            n_mm = 2 - s % 2
            nc.tensor.matmul(
                out=pos[s][:, : n_mm * P],
                lhsT=ones_row[:],
                rhs=beta_row[:, : n_mm * P],
                start=False,
                stop=False,
            )
            for c in range(n_mm, 4):
                nc.tensor.matmul(
                    out=pos[s][:, c * P : (c + 1) * P],
                    lhsT=betacol[:, c, :],
                    rhs=ident_f[:],
                    is_transpose=True,
                    start=False,
                    stop=(c == 3),
                )

        def add_x(s):
            if not 0 <= s < B:
                return
            q, i = s // QUAD, s % QUAD
            if i == 0:
                xb[q] = w3.tile([P, QUAD, D], F32, name="xb", tag="xb")
            nc.vector.tensor_tensor(
                out=xb[q][:, i, :], in0=mx[s][:], in1=xq[q][:, i * D : (i + 1) * D], op=ALU.add
            )

        def add_pos(s):
            if not 0 <= s < B:
                return
            q, i, j = s // QUAD, s % QUAD, s // 2
            if s % 2 == 0:
                sums[j] = w4.tile([P, 2], F32, name="sums", tag="sums")
            nc.vector.scalar_tensor_tensor(
                out=xb[q][:, i, :],
                in0=pos[s][:],
                scalar=1.0,
                in1=xb[q][:, i, :],
                op0=ALU.mult,
                op1=ALU.add,
                accum_out=sums[j][:, s % 2 : s % 2 + 1],
            )

        def minus_mean(j):
            if not 0 <= j < NPAIR:
                return
            nm[j] = w4.tile([P, 2], F32, name="nm", tag="nm")
            nc.scalar.activation(out=nm[j][:], in_=sums[j][:], func=ACT.Copy, scale=-1.0 / D)

        def squares(j):
            if not 0 <= j < NPAIR:
                return
            ssq[j] = w4.tile([P, 2], F32, name="ssq", tag="ssq")
            for e in range(2):
                s = 2 * j + e
                junk = w2.tile([P, D], BF16, name="junk", tag="junk")
                nc.scalar.activation(
                    out=junk[:],
                    in_=xb[s // QUAD][:, s % QUAD, :],
                    func=ACT.Square,
                    bias=nm[j][:, e : e + 1],
                    scale=1.0,
                    accum_out=ssq[j][:, e : e + 1],
                )

        def normalise(j):
            if not 0 <= j < NPAIR:
                return
            q = j // 2
            var = w4.tile([P, 2], F32, name="var", tag="var")
            nc.gpsimd.tensor_scalar(
                out=var[:], in0=ssq[j][:], scalar1=1.0 / D, scalar2=EPS, op0=ALU.mult, op1=ALU.add
            )
            rstd[j] = w4.tile([P, 2], F32, name="rstd", tag="rstd")
            nc.gpsimd.tensor_tensor(out=rstd[j][:], in0=var[:], in1=mhalf[:], op=ALU.pow)
            if j % 2 == 0:
                z[q] = w3.tile([P, QUAD, D], F32, name="z", tag="z")
            for e in range(2):
                i = 2 * (j % 2) + e
                nc.gpsimd.tensor_scalar(
                    out=z[q][:, i, :],
                    in0=xb[q][:, i, :],
                    scalar1=nm[j][:, e : e + 1],
                    scalar2=rstd[j][:, e : e + 1],
                    op0=ALU.add,
                    op1=ALU.mult,
                )

        def z_transposes(q, t):
            if not 0 <= q < NQ:
                return
            zt[q, t] = ps_tr.tile([P, QUAD, P], F32, name="zt", tag="tr")
            for i in range(QUAD):
                nc.tensor.transpose(zt[q, t][:, i, :], z[q][:, i, t * P : (t + 1) * P], ident_f[:])

        def gain_bias(q, t):
            if not 0 <= q < NQ:
                return
            if t == 0:
                planes[q] = w2.tile([P, 4, QUAD * P], BF16, name="planes", tag="planes")
            nc.scalar.activation(
                out=planes[q][:, t, :],
                in_=zt[q, t][:].rearrange("p s n -> p (s n)"),
                func=ACT.Identity,
                bias=bT[:, t : t + 1],
                scale=gT[:, t : t + 1],
            )

        def regroup_scalar(j):
            if not 0 <= j < NPAIR:
                return
            w0 = (j % 2) * PAIR_W
            g2[j] = w3.tile([P, PAIR_W, 4], BF16, name="g2", tag="g2", align_bytes=64)
            regroup(
                nc.scalar.copy, g2[j][:, RG_V:, :], planes[j // 2][:, :, w0 + RG_V : w0 + PAIR_W]
            )

        def regroup_vector(j):
            if not 0 <= j < NPAIR:
                return
            w0 = (j % 2) * PAIR_W
            regroup(nc.vector.tensor_copy, g2[j][:, :RG_V, :], planes[j // 2][:, :, w0 : w0 + RG_V])

        def h_quantise(j):
            if not 0 <= j < NPAIR:
                return
            c2[j] = w3.tile([P, PAIR_W], U32, name="c2", tag="c2", align_bytes=64)
            s2[j] = w3.tile([P, PAIR_W], U8, name="s2", tag="s2", align_bytes=64)
            nc.vector.quantize_mx(
                out=c2[j][:].bitcast(FP8X4),
                scales=s2[j][:],
                in_=g2[j][:].rearrange("p w t -> p (w t)"),
            )

        def mlp_matmul(j):
            if not 0 <= j < NPAIR:
                return
            m2[j] = ps_mm.tile([P, 2, HID], F32, name="m2", tag="mm")
            for e in range(2):
                nc.tensor.matmul_mx(
                    out=m2[j][:, e, :],
                    lhsT=c2[j][:, e * P : (e + 1) * P].bitcast(FP8X4),
                    lhsT_scale=s2[j][:, e * P : (e + 1) * P],
                    rhs=w1cod[:].bitcast(FP8X4),
                    rhs_scale=w1sc[:],
                    start=True,
                    stop=True,
                )

        def mlp_bias(j):
            if not 0 <= j < NPAIR:
                return
            o[j] = w2.tile([P, 2, HID], F32, name="o", tag="o")
            nc.vector.tensor_tensor(
                out=o[j][:],
                in0=m2[j][:],
                in1=b1bc[:].unsqueeze(1).to_broadcast([P, 2, HID]),
                op=ALU.add,
            )

        def gelu_store(j):
            if not 0 <= j < NPAIR:
                return
            res = w3.tile([P, 2, HID], F32, name="res", tag="res")
            nc.scalar.activation(out=res[:], in_=o[j][:], func=ACT.Gelu_apprx_tanh)
            nc.sync.dma_start(out=out_v[:, 2 * j : 2 * j + 2, :], in_=res[:])

        ctx.enter_context(tc.manual_schedule(engines={mybir.EngineType.PE, mybir.EngineType.DVE, mybir.EngineType.Activation, mybir.EngineType.Pool}))
        for j in range(-4, NPAIR + 10):
            if j >= 0 and j % 2 == 0:
                load_h(j // 2 + 5)
                load_x(j // 2 + 3)
            mlp_matmul(j - 8)
            feat_matmul(2 * j + 2)
            feat_matmul(2 * j + 3)
            z_transposes((j - 4) // 2, 2 * ((j - 4) % 2))
            z_transposes((j - 4) // 2, 2 * ((j - 4) % 2) + 1)
            h2_transposes(j + 4)
            pos_matmul(2 * j + 2)
            pos_matmul(2 * j + 3)
            regroup_vector(j - 7)
            mlp_bias(j - 9)
            add_x(2 * j)
            add_x(2 * j + 1)
            add_pos(2 * j)
            add_pos(2 * j + 1)
            h2_quantise(j + 2)
            h_quantise(j - 7)
            if j == 1:
                quantise_w1()
            minus_mean(j - 1)
            gain_bias((j - 5) // 2, 2 * ((j - 5) % 2))
            gain_bias((j - 5) // 2, 2 * ((j - 5) % 2) + 1)
            h2_copy(j + 3)
            squares(j - 1)
            gelu_store(j - 9)
            regroup_scalar(j - 6)
            normalise(j - 1)
